import numpy as np
import ml_dtypes


def mxq(x, axis, fmt="e4m3"):
    dtype, down = {"e4m3": (ml_dtypes.float8_e4m3fn, 7), "e5m2": (ml_dtypes.float8_e5m2, 14)}[fmt]
    v = np.moveaxis(np.asarray(x, np.float32).astype(ml_dtypes.bfloat16).astype(np.float64), axis, -1)
    blocks = v.reshape(v.shape[:-1] + (-1, 32))
    amax = np.abs(blocks).max(-1, keepdims=True)
    byte = np.maximum(np.where(amax > 0, np.frexp(amax)[1] - 1 + 127, 0) - down, 1)
    scale = np.exp2(byte - 127.0)
    codes = (blocks / scale).astype(np.float32).astype(dtype).astype(np.float64)
    return np.moveaxis((codes * scale).reshape(v.shape), -1, axis)


WIDE = False


def mx_kscale(k):
    if not WIDE:
        return np.ones(k)
    levels = np.array([10, -10, 5, -5, 0])
    a = np.random.permutation(np.resize(levels, k // 512 * 4)).reshape(k // 512, 4)
    idx = np.arange(k)
    return np.exp2(a[idx // 512, idx % 128 // 32])


BF16 = ml_dtypes.bfloat16


def bf(x):
    return np.asarray(x, np.float32).astype(BF16)


def f64(x):
    return np.asarray(x).astype(np.float64)


B, IN, H = 384, 512, 1024


def sigmoid(v):
    return 1.0 / (1.0 + np.exp(-v))


def setup_inputs():
    s = mx_kscale(IN)
    return {
        "inputs": bf(np.random.standard_normal((B, IN)) * s),
        "h0": bf(np.random.standard_normal((B, H)) * 0.5),
        "c0": bf(np.random.standard_normal((B, H))),
        "w_ih": bf(np.random.standard_normal((4 * H, IN)) / np.sqrt(IN) / s),
        "w_hh": bf(np.random.standard_normal((4 * H, H)) * 2.0 / np.sqrt(H)),
        "b_ih": bf(np.random.standard_normal(4 * H) * 0.3),
        "b_hh": bf(np.random.standard_normal(4 * H) * 0.3),
    }


def lstm_cell(xq, h, c, wihq, whhq, b_ih, b_hh):
    gates = (xq @ wihq.T) + (mxq(h, 1, "e4m3") @ whhq.T) + b_ih + b_hh
    i, f, g, o = np.split(gates, 4, axis=-1)
    i, f, o = sigmoid(i), sigmoid(f), sigmoid(o)
    g = np.tanh(g)
    c_new = f * c + i * g
    h_new = o * np.tanh(c_new)
    return h_new, c_new


def reference(inputs, h0, c0, w_ih, w_hh, b_ih, b_hh):
    xq = mxq(f64(inputs), 1, "e4m3")
    wihq = mxq(f64(w_ih), 1, "e4m3")
    whhq = mxq(f64(w_hh), 1, "e4m3")
    b_ih, b_hh = f64(b_ih), f64(b_hh)
    h, c = lstm_cell(xq, f64(h0), f64(c0), wihq, whhq, b_ih, b_hh)
    h, c = lstm_cell(xq, h, c, wihq, whhq, b_ih, b_hh)
    return (h, c)

@@ -1,0 +1,243 @@
+from contextlib import ExitStack
+
+import concourse.mybir as mybir
+from concourse.masks import make_identity
+
+F32 = mybir.dt.float32
+BF16 = mybir.dt.bfloat16
+U32 = mybir.dt.uint32
+U8 = mybir.dt.uint8
+FP8X4 = mybir.dt.float8_e4m3fn_x4
+ACT = mybir.ActivationFunctionType
+ALU = mybir.AluOpType
+
+P = 128
+NB = 384
+UNITS = 8
+FLOPS = 2 * 2 * 384 * 4096 * 1536
+N_SPLIT = ((0, 256), (256, 384))
+EVAC = "SVSSVS"
+PINNED = False
+
+
+def tile_odelstmcell_pa_kernel(tc, inputs, h0, c0, w_ih, w_hh, b_ih, b_hh, out_0, out_1):
+    nc = tc.nc
+    with ExitStack() as ctx:
+        const = ctx.enter_context(tc.tile_pool(name="const", bufs=1))
+        rawp = ctx.enter_context(tc.tile_pool(name="rawp", bufs=2))
+        grpp = ctx.enter_context(tc.tile_pool(name="grpp", bufs=4))
+        iop = ctx.enter_context(tc.tile_pool(name="iop", bufs=3))
+        gact = ctx.enter_context(tc.tile_pool(name="gact", bufs=3))
+        h2p = ctx.enter_context(tc.tile_pool(name="h2p", bufs=4))
+        psum_t = ctx.enter_context(tc.psum_pool(name="psum_t", bufs=4))
+        psum_g = ctx.enter_context(tc.psum_pool(name="psum_g", bufs=4))
+        if PINNED:
+            ctx.enter_context(tc.manual_schedule())
+
+        def evac(who, out, in_):
+            if who == "S":
+                nc.scalar.copy(out=out, in_=in_)
+            else:
+                nc.vector.tensor_copy(out=out, in_=in_)
+
+        warm = const.tile([P, 1], F32)
+        nc.vector.memset(warm[:], 0.0)
+        nc.scalar.activation(out=warm[:], in_=warm[:], func=ACT.Sigmoid)
+        ident = const.tile([P, P], F32)
+        make_identity(nc, ident[:])
+        bias_raw = const.tile([P, 256], BF16)
+        nc.vector.memset(bias_raw[:], 0.0)
+
+        x_raw = iop.tile([P, 3 * 512], BF16, tag="io")
+        nc.sync.dma_start(out=x_raw[:], in_=inputs.rearrange("(p t) k -> p (t k)", t=3))
+        h0_raw = iop.tile([P, 3 * 1024], BF16, tag="io")
+        nc.sync.dma_start(out=h0_raw[:], in_=h0.rearrange("(p t) k -> p (t k)", t=3))
+        nc.scalar.dma_start(out=bias_raw[0:16, :], in_=b_ih.rearrange("(r c) -> r c", c=256))
+        nc.scalar.dma_start(out=bias_raw[16:32, :], in_=b_hh.rearrange("(r c) -> r c", c=256))
+        wih_v = w_ih.rearrange("(g b p e) k -> b p g (e k)", g=4, b=4, p=P, e=2)
+        whh_v = w_hh.rearrange("(g b p e) k -> b p g (e k)", g=4, b=4, p=P, e=2)
+        wih_f = []
+        whh_f = []
+        c0_raw = None
+        for b in range(4):
+            wih_raw = rawp.tile([P, 4096], BF16, tag="wih")
+            nc.sync.dma_start(out=wih_raw[:].rearrange("p (g r) -> p g r", g=4), in_=wih_v[b])
+            whh_raw = rawp.tile([P, 8192], BF16, tag="whh")
+            nc.sync.dma_start(out=whh_raw[:].rearrange("p (g r) -> p g r", g=4), in_=whh_v[b])
+            wih_f.append(wih_raw[:].bitcast(F32).rearrange("p (g e w) -> p g e w", g=4, e=2))
+            whh_f.append(whh_raw[:].bitcast(F32).rearrange("p (g e w) -> p g e w", g=4, e=2))
+            if b == 0:
+                c0_raw = iop.tile([P, 3 * 1024], BF16, tag="io")
+                nc.sync.dma_start(out=c0_raw[:], in_=c0.rearrange("(p t) k -> p (t k)", t=3))
+        x_f = x_raw[:].bitcast(F32).rearrange("p (t w) -> p t w", t=3)
+        h0_f = h0_raw[:].bitcast(F32).rearrange("p (t w) -> p t w", t=3)
+        c0_f = c0_raw[:].bitcast(F32).rearrange("p (t w) -> p t w", t=3)
+
+        a_grp = const.tile([P, 3 * NB * 2], F32, align_bytes=64)
+        a_grp5 = a_grp[:].rearrange("p (s t m u) -> p s t m u", s=3, t=3, u=2)
+        a_bf = a_grp[:].bitcast(BF16)
+        a_codes = const.tile([P, 3 * NB], U32, align_bytes=64)
+        a_scales = const.tile([P, 3 * NB], U8, align_bytes=64)
+        h1_pl = const.tile([P, 2, 4, NB], BF16)
+        h1_grp = const.tile([P, 2, NB, 4], BF16, align_bytes=64)
+        h1_flat = h1_grp[:].rearrange("p g n t -> p (g n t)")
+        h1_codes = const.tile([P, 2 * NB], U32, align_bytes=64)
+        h1_scales = const.tile([P, 2 * NB], U8, align_bytes=64)
+        c0T = const.tile([P, 4 * NB], F32)
+        c0T_bf = c0T[:].bitcast(BF16).rearrange("p (b n e) -> p b n e", b=4, e=2)
+        c_st = const.tile([P, UNITS, NB], F32)
+        w_codes = const.tile([P, 96 * P], U32, align_bytes=64)
+        w_scales = const.tile([P, 96 * P], U8, align_bytes=64)
+        bias_w = const.tile([P, 32], F32)
+        bias = const.tile([P, 32], F32)
+
+        for s in range(3):
+            for t0, nt in ((0, 2), (2, 1)):
+                tp = psum_t.tile([P, 2, 2, P], F32, tag="tp")
+                for tl in range(nt):
+                    for u in range(2):
+                        if s == 0:
+                            src = x_f[:, t0 + tl, 128 * u : 128 * u + 128]
+                        else:
+                            lo = 256 * (s - 1) + 128 * u
+                            src = h0_f[:, t0 + tl, lo : lo + 128]
+                        nc.tensor.transpose(tp[:, tl, u, :], src, ident[:])
+                evac(
+                    "V" if nt == 2 else "S",
+                    a_grp5[:, s, t0 : t0 + nt],
+                    tp[:, 0:nt].rearrange("p t u m -> p t m u"),
+                )
+            for n0, n1 in N_SPLIT:
+                nc.vector.quantize_mx(
+                    out=a_codes[:, s * NB + n0 : s * NB + n1].bitcast(FP8X4),
+                    scales=a_scales[:, s * NB + n0 : s * NB + n1],
+                    in_=a_bf[:, 4 * (s * NB + n0) : 4 * (s * NB + n1)],
+                )
+
+        tp = psum_t.tile([P, 2, 2, P], F32, tag="tp")
+        nc.tensor.transpose(tp[:, 0, 0, :], bias_raw[:].bitcast(F32), ident[:])
+        nc.vector.tensor_copy(out=bias_w[:], in_=tp[:, 0, 0, 0:32])
+        bias_wb = bias_w[:].bitcast(BF16)
+        nc.vector.tensor_tensor(out=bias[:], in0=bias_wb[:, 0:32], in1=bias_wb[:, 32:64], op=ALU.add)
+
+        def weight_unit(j):
+            b, e = divmod(j, 2)
+            for s in range(3):
+                grp = grpp.tile([P, 1024], F32, tag="grp", align_bytes=64)
+                grp4 = grp[:].rearrange("p (g m u) -> p g m u", g=4, u=2)
+                for half in range(2):
+                    tp = psum_t.tile([P, 2, 2, P], F32, tag="tp")
+                    for gl in range(2):
+                        for u in range(2):
+                            if s == 0:
+                                src = wih_f[b][:, 2 * half + gl, e, 128 * u : 128 * u + 128]
+                            else:
+                                lo = 256 * (s - 1) + 128 * u
+                                src = whh_f[b][:, 2 * half + gl, e, lo : lo + 128]
+                            nc.tensor.transpose(tp[:, gl, u, :], src, ident[:])
+                    evac(
+                        EVAC[2 * s + half],
+                        grp4[:, 2 * half : 2 * half + 2],
+                        tp[:].rearrange("p g u m -> p g m u"),
+                    )
+                base = (j * 3 + s) * 4 * P
+                nc.vector.quantize_mx(
+                    out=w_codes[:, base : base + 4 * P].bitcast(FP8X4),
+                    scales=w_scales[:, base : base + 4 * P],
+                    in_=grp[:].bitcast(BF16),
+                )
+
+        def c0_prep():
+            for b in range(4):
+                tp = psum_t.tile([P, 512], F32, tag="tp")
+                for t in range(3):
+                    nc.tensor.transpose(tp[:, 128 * t : 128 * t + 128], c0_f[:, t, 128 * b : 128 * b + 128], ident[:])
+                evac("SV"[b % 2], c0T[:, NB * b : NB * b + NB], tp[:, 0:NB])
+
+        def gates_mx(j, cell):
+            gates = []
+            for gi in range(4):
+                gt = psum_g.tile([P, NB], F32, tag="gate")
+                for n0, n1 in N_SPLIT:
+                    for s in range(3):
+                        col = ((j * 3 + s) * 4 + gi) * P
+                        if s == 0 or cell == 0:
+                            rc, rs, off = a_codes, a_scales, s * NB
+                        else:
+                            rc, rs, off = h1_codes, h1_scales, (s - 1) * NB
+                        nc.tensor.matmul_mx(
+                            out=gt[:, n0:n1],
+                            lhsT=w_codes[:, col : col + P].bitcast(FP8X4),
+                            lhsT_scale=w_scales[:, col : col + P],
+                            rhs=rc[:, off + n0 : off + n1].bitcast(FP8X4),
+                            rhs_scale=rs[:, off + n0 : off + n1],
+                            start=(s == 0),
+                            stop=(s == 2),
+                        )
+                gates.append(gt)
+            return gates
+
+        def epilogue(j, cell, gates):
+            b, e = divmod(j, 2)
+            acts = []
+            for gi in range(4):
+                a = gact.tile([P, NB], F32, tag="a%d" % gi)
+                nc.scalar.activation(
+                    out=a[:],
+                    in_=gates[gi][:],
+                    func=ACT.Tanh if gi == 2 else ACT.Sigmoid,
+                    bias=bias[:, 8 * gi + j : 8 * gi + j + 1],
+                )
+                acts.append(a)
+            ai, af, ag, ao = acts
+            cprev = c0T_bf[:, b, :, e] if cell == 0 else c_st[:, j, :]
+            nc.vector.tensor_tensor(out=af[:], in0=af[:], in1=cprev, op=ALU.mult)
+            nc.vector.tensor_tensor(out=ai[:], in0=ai[:], in1=ag[:], op=ALU.mult)
+            nc.vector.tensor_tensor(out=c_st[:, j, :], in0=af[:], in1=ai[:], op=ALU.add)
+            nc.scalar.activation(out=ag[:], in_=c_st[:, j, :], func=ACT.Tanh)
+            if cell == 0:
+                nc.vector.tensor_tensor(out=h1_pl[:, j // 4, j % 4, :], in0=ao[:], in1=ag[:], op=ALU.mult)
+                return None
+            h2 = h2p.tile([P, NB], F32, tag="h2")
+            nc.vector.tensor_tensor(out=h2[:], in0=ao[:], in1=ag[:], op=ALU.mult)
+            return h2
+
+        def h1_quant(g):
+            nc.vector.tensor_copy(out=h1_grp[:, g], in_=h1_pl[:, g].rearrange("p t n -> p n t"))
+            for n0, n1 in N_SPLIT:
+                nc.vector.quantize_mx(
+                    out=h1_codes[:, g * NB + n0 : g * NB + n1].bitcast(FP8X4),
+                    scales=h1_scales[:, g * NB + n0 : g * NB + n1],
+                    in_=h1_flat[:, 4 * (g * NB + n0) : 4 * (g * NB + n1)],
+                )
+
+        out_h = out_0.rearrange("(p t) h -> p t h", t=3)
+        out_c = out_1.rearrange("(p t) h -> p t h", t=3)
+
+        def outputs(b, h2_pair):
+            o_sb = iop.tile([P, 2, 3, 256], F32, tag="io")
+            o5 = o_sb[:].rearrange("p w t (m e) -> p w t m e", e=2)
+            for t in range(3):
+                ot = psum_t.tile([P, 2, 2, P], F32, tag="tp")
+                for e in range(2):
+                    nc.tensor.transpose(ot[:, 0, e, :], c_st[:, 2 * b + e, 128 * t : 128 * t + 128], ident[:])
+                    nc.tensor.transpose(ot[:, 1, e, :], h2_pair[e][:, 128 * t : 128 * t + 128], ident[:])
+                nc.vector.tensor_copy(out=o5[:, :, t], in_=ot[:].rearrange("p w e m -> p w m e"))
+            nc.sync.dma_start(out=out_c[:, :, 256 * b : 256 * b + 256], in_=o_sb[:, 0])
+            nc.sync.dma_start(out=out_h[:, :, 256 * b : 256 * b + 256], in_=o_sb[:, 1])
+
+        weight_unit(0)
+        c0_prep()
+        for j in range(UNITS):
+            if j + 1 < UNITS:
+                weight_unit(j + 1)
+            epilogue(j, 0, gates_mx(j, 0))
+            if j == 3:
+                h1_quant(0)
+        h1_quant(1)
+        pair = []
+        for j in range(UNITS):
+            pair.append(epilogue(j, 1, gates_mx(j, 1)))
+            if j % 2 == 1:
+                outputs(j // 2, pair)
+                pair = []

@@ -14,25 +14,26 @@ ALU = mybir.AluOpType
 P = 128
 NB = 384
 UNITS = 8
+HALVES = 2 * UNITS
 FLOPS = 2 * 2 * 384 * 4096 * 1536
 N_SPLIT = ((0, 256), (256, 384))
-EVAC = "SVSSVS"
-PINNED = False
+RAW_BUFS = 8
+OUT_DELAY = 2
+PRE_UNITS = 2
+GATE_FUNC = (ACT.Sigmoid, ACT.Sigmoid, ACT.Tanh, ACT.Sigmoid)
 
 
 def tile_odelstmcell_pa_kernel(tc, inputs, h0, c0, w_ih, w_hh, b_ih, b_hh, out_0, out_1):
     nc = tc.nc
     with ExitStack() as ctx:
         const = ctx.enter_context(tc.tile_pool(name="const", bufs=1))
-        rawp = ctx.enter_context(tc.tile_pool(name="rawp", bufs=2))
-        grpp = ctx.enter_context(tc.tile_pool(name="grpp", bufs=4))
-        iop = ctx.enter_context(tc.tile_pool(name="iop", bufs=3))
+        rawp = ctx.enter_context(tc.tile_pool(name="rawp", bufs=RAW_BUFS))
+        grpp = ctx.enter_context(tc.tile_pool(name="grpp", bufs=6))
         gact = ctx.enter_context(tc.tile_pool(name="gact", bufs=3))
         h2p = ctx.enter_context(tc.tile_pool(name="h2p", bufs=4))
-        psum_t = ctx.enter_context(tc.psum_pool(name="psum_t", bufs=4))
-        psum_g = ctx.enter_context(tc.psum_pool(name="psum_g", bufs=4))
-        if PINNED:
-            ctx.enter_context(tc.manual_schedule())
+        outp = ctx.enter_context(tc.tile_pool(name="outp", bufs=4))
+        psum = ctx.enter_context(tc.psum_pool(name="psum", bufs=8))
+        ctx.enter_context(tc.manual_schedule())
 
         def evac(who, out, in_):
             if who == "S":
@@ -48,26 +49,36 @@ def tile_odelstmcell_pa_kernel(tc, inputs, h0, c0, w_ih, w_hh, b_ih, b_hh, out_0
         bias_raw = const.tile([P, 256], BF16)
         nc.vector.memset(bias_raw[:], 0.0)
 
-        x_raw = iop.tile([P, 3 * 512], BF16, tag="io")
+        x_raw = const.tile([P, 3 * 512], BF16)
         nc.sync.dma_start(out=x_raw[:], in_=inputs.rearrange("(p t) k -> p (t k)", t=3))
-        h0_raw = iop.tile([P, 3 * 1024], BF16, tag="io")
+        h0_raw = const.tile([P, 3 * 1024], BF16)
         nc.sync.dma_start(out=h0_raw[:], in_=h0.rearrange("(p t) k -> p (t k)", t=3))
         nc.scalar.dma_start(out=bias_raw[0:16, :], in_=b_ih.rearrange("(r c) -> r c", c=256))
         nc.scalar.dma_start(out=bias_raw[16:32, :], in_=b_hh.rearrange("(r c) -> r c", c=256))
-        wih_v = w_ih.rearrange("(g b p e) k -> b p g (e k)", g=4, b=4, p=P, e=2)
-        whh_v = w_hh.rearrange("(g b p e) k -> b p g (e k)", g=4, b=4, p=P, e=2)
-        wih_f = []
-        whh_f = []
-        c0_raw = None
-        for b in range(4):
-            wih_raw = rawp.tile([P, 4096], BF16, tag="wih")
-            nc.sync.dma_start(out=wih_raw[:].rearrange("p (g r) -> p g r", g=4), in_=wih_v[b])
-            whh_raw = rawp.tile([P, 8192], BF16, tag="whh")
-            nc.sync.dma_start(out=whh_raw[:].rearrange("p (g r) -> p g r", g=4), in_=whh_v[b])
-            wih_f.append(wih_raw[:].bitcast(F32).rearrange("p (g e w) -> p g e w", g=4, e=2))
-            whh_f.append(whh_raw[:].bitcast(F32).rearrange("p (g e w) -> p g e w", g=4, e=2))
-            if b == 0:
-                c0_raw = iop.tile([P, 3 * 1024], BF16, tag="io")
+        c0_raw = const.tile([P, 3 * 1024], BF16)
+        wih_v = w_ih.rearrange("(g b p e) k -> b e p g k", g=4, b=4, p=P, e=2)
+        whh_v = w_hh.rearrange("(g b p e) k -> b e p g k", g=4, b=4, p=P, e=2)
+        raw_views = {}
+
+        def load_half(hh):
+            j, hf = divmod(hh, 2)
+            b, e = divmod(j, 2)
+            wih_raw = rawp.tile([P, 2 * 512], BF16, tag="wih")
+            nc.sync.dma_start(
+                out=wih_raw[:].rearrange("p (g k) -> p g k", g=2), in_=wih_v[b, e][:, 2 * hf : 2 * hf + 2, :]
+            )
+            whh_raw = rawp.tile([P, 2 * 1024], BF16, tag="whh")
+            nc.sync.dma_start(
+                out=whh_raw[:].rearrange("p (g k) -> p g k", g=2), in_=whh_v[b, e][:, 2 * hf : 2 * hf + 2, :]
+            )
+            raw_views[hh] = (
+                wih_raw[:].bitcast(F32).rearrange("p (g w) -> p g w", g=2),
+                whh_raw[:].bitcast(F32).rearrange("p (g w) -> p g w", g=2),
+            )
+
+        for hh in range(RAW_BUFS):
+            load_half(hh)
+            if hh == 2:
                 nc.sync.dma_start(out=c0_raw[:], in_=c0.rearrange("(p t) k -> p (t k)", t=3))
         x_f = x_raw[:].bitcast(F32).rearrange("p (t w) -> p t w", t=3)
         h0_f = h0_raw[:].bitcast(F32).rearrange("p (t w) -> p t w", t=3)
@@ -93,7 +104,7 @@ def tile_odelstmcell_pa_kernel(tc, inputs, h0, c0, w_ih, w_hh, b_ih, b_hh, out_0
 
         for s in range(3):
             for t0, nt in ((0, 2), (2, 1)):
-                tp = psum_t.tile([P, 2, 2, P], F32, tag="tp")
+                tp = psum.tile([P, 2, 2, P], F32, tag="bank")
                 for tl in range(nt):
                     for u in range(2):
                         if s == 0:
@@ -114,130 +125,202 @@ def tile_odelstmcell_pa_kernel(tc, inputs, h0, c0, w_ih, w_hh, b_ih, b_hh, out_0
                     in_=a_bf[:, 4 * (s * NB + n0) : 4 * (s * NB + n1)],
                 )
 
-        tp = psum_t.tile([P, 2, 2, P], F32, tag="tp")
+        tp = psum.tile([P, 2, 2, P], F32, tag="bank")
         nc.tensor.transpose(tp[:, 0, 0, :], bias_raw[:].bitcast(F32), ident[:])
         nc.vector.tensor_copy(out=bias_w[:], in_=tp[:, 0, 0, 0:32])
         bias_wb = bias_w[:].bitcast(BF16)
         nc.vector.tensor_tensor(out=bias[:], in0=bias_wb[:, 0:32], in1=bias_wb[:, 32:64], op=ALU.add)
 
-        def weight_unit(j):
-            b, e = divmod(j, 2)
-            for s in range(3):
-                grp = grpp.tile([P, 1024], F32, tag="grp", align_bytes=64)
-                grp4 = grp[:].rearrange("p (g m u) -> p g m u", g=4, u=2)
-                for half in range(2):
-                    tp = psum_t.tile([P, 2, 2, P], F32, tag="tp")
-                    for gl in range(2):
-                        for u in range(2):
-                            if s == 0:
-                                src = wih_f[b][:, 2 * half + gl, e, 128 * u : 128 * u + 128]
-                            else:
-                                lo = 256 * (s - 1) + 128 * u
-                                src = whh_f[b][:, 2 * half + gl, e, lo : lo + 128]
-                            nc.tensor.transpose(tp[:, gl, u, :], src, ident[:])
-                    evac(
-                        EVAC[2 * s + half],
-                        grp4[:, 2 * half : 2 * half + 2],
-                        tp[:].rearrange("p g u m -> p g m u"),
-                    )
-                base = (j * 3 + s) * 4 * P
-                nc.vector.quantize_mx(
-                    out=w_codes[:, base : base + 4 * P].bitcast(FP8X4),
-                    scales=w_scales[:, base : base + 4 * P],
-                    in_=grp[:].bitcast(BF16),
-                )
+        def transposes(hh):
+            wih_f, whh_f = raw_views[hh]
+            banks = []
+            for k in range(3):
+                tp = psum.tile([P, 2, 2, P], F32, tag="bank")
+                for i in range(2):
+                    gl, s = divmod(2 * k + i, 3)
+                    for u in range(2):
+                        if s == 0:
+                            src = wih_f[:, gl, 128 * u : 128 * u + 128]
+                        else:
+                            lo = 256 * (s - 1) + 128 * u
+                            src = whh_f[:, gl, lo : lo + 128]
+                        nc.tensor.transpose(tp[:, i, u, :], src, ident[:])
+                banks.append(tp)
+            return banks
+
+        def evac_bank(who, bank):
+            grp = grpp.tile([P, 512], F32, tag="grp", align_bytes=64)
+            evac(who, grp[:].rearrange("p (i m u) -> p i m u", i=2, u=2), bank[:].rearrange("p i u m -> p i m u"))
+            return grp
+
+        def quantise_bank(hh, k, grp):
+            base = (hh * 6 + 2 * k) * P
+            nc.vector.quantize_mx(
+                out=w_codes[:, base : base + 2 * P].bitcast(FP8X4),
+                scales=w_scales[:, base : base + 2 * P],
+                in_=grp[:].bitcast(BF16),
+            )
+
+        def evac_quantise(hh, banks, between):
+            g0 = evac_bank("S", banks[0])
+            g1 = evac_bank("V", banks[1])
+            if between is not None:
+                between()
+            quantise_bank(hh, 0, g0)
+            quantise_bank(hh, 1, g1)
+            g2 = evac_bank("S", banks[2])
+            quantise_bank(hh, 2, g2)
 
         def c0_prep():
             for b in range(4):
-                tp = psum_t.tile([P, 512], F32, tag="tp")
+                tp = psum.tile([P, 512], F32, tag="bank")
                 for t in range(3):
                     nc.tensor.transpose(tp[:, 128 * t : 128 * t + 128], c0_f[:, t, 128 * b : 128 * b + 128], ident[:])
                 evac("SV"[b % 2], c0T[:, NB * b : NB * b + NB], tp[:, 0:NB])
 
-        def gates_mx(j, cell):
-            gates = []
-            for gi in range(4):
-                gt = psum_g.tile([P, NB], F32, tag="gate")
-                for n0, n1 in N_SPLIT:
-                    for s in range(3):
-                        col = ((j * 3 + s) * 4 + gi) * P
-                        if s == 0 or cell == 0:
-                            rc, rs, off = a_codes, a_scales, s * NB
-                        else:
-                            rc, rs, off = h1_codes, h1_scales, (s - 1) * NB
-                        nc.tensor.matmul_mx(
-                            out=gt[:, n0:n1],
-                            lhsT=w_codes[:, col : col + P].bitcast(FP8X4),
-                            lhsT_scale=w_scales[:, col : col + P],
-                            rhs=rc[:, off + n0 : off + n1].bitcast(FP8X4),
-                            rhs_scale=rs[:, off + n0 : off + n1],
-                            start=(s == 0),
-                            stop=(s == 2),
-                        )
-                gates.append(gt)
-            return gates
-
-        def epilogue(j, cell, gates):
-            b, e = divmod(j, 2)
-            acts = []
-            for gi in range(4):
-                a = gact.tile([P, NB], F32, tag="a%d" % gi)
-                nc.scalar.activation(
-                    out=a[:],
-                    in_=gates[gi][:],
-                    func=ACT.Tanh if gi == 2 else ACT.Sigmoid,
-                    bias=bias[:, 8 * gi + j : 8 * gi + j + 1],
+        def passes(gt, j, gi, cell, part, which):
+            n0, n1 = N_SPLIT[part]
+            for s in which:
+                col = (j * 12 + gi * 3 + s) * P
+                if s == 0 or cell == 0:
+                    rc, rs, off = a_codes, a_scales, s * NB
+                else:
+                    rc, rs, off = h1_codes, h1_scales, (s - 1) * NB
+                nc.tensor.matmul_mx(
+                    out=gt[:, n0:n1],
+                    lhsT=w_codes[:, col : col + P].bitcast(FP8X4),
+                    lhsT_scale=w_scales[:, col : col + P],
+                    rhs=rc[:, off + n0 : off + n1].bitcast(FP8X4),
+                    rhs_scale=rs[:, off + n0 : off + n1],
+                    start=(s == 0),
+                    stop=(s == 2),
                 )
-                acts.append(a)
-            ai, af, ag, ao = acts
-            cprev = c0T_bf[:, b, :, e] if cell == 0 else c_st[:, j, :]
+
+        gates = {}
+        acts = {}
+
+        def gate_mx(j, gi, cell):
+            gt = psum.tile([P, NB], F32, tag="bank")
+            passes(gt, j, gi, cell, 0, (0, 1, 2))
+            passes(gt, j, gi, cell, 1, (0, 1, 2))
+            gates[(cell, j, gi)] = gt
+
+        def gate_act(j, gi, cell):
+            a = gact.tile([P, NB], F32, tag="a%d" % gi)
+            nc.scalar.activation(
+                out=a[:],
+                in_=gates[(cell, j, gi)][:],
+                func=GATE_FUNC[gi],
+                bias=bias[:, 8 * gi + j : 8 * gi + j + 1],
+            )
+            acts[(cell, j, gi)] = a
+
+        def mul_fc(j, cell):
+            af = acts[(cell, j, 1)]
+            cprev = c0T_bf[:, j // 2, :, j % 2] if cell == 0 else c_st[:, j, :]
             nc.vector.tensor_tensor(out=af[:], in0=af[:], in1=cprev, op=ALU.mult)
-            nc.vector.tensor_tensor(out=ai[:], in0=ai[:], in1=ag[:], op=ALU.mult)
-            nc.vector.tensor_tensor(out=c_st[:, j, :], in0=af[:], in1=ai[:], op=ALU.add)
-            nc.scalar.activation(out=ag[:], in_=c_st[:, j, :], func=ACT.Tanh)
+
+        def mul_ig(j, cell):
+            ai = acts[(cell, j, 0)]
+            nc.vector.tensor_tensor(out=ai[:], in0=ai[:], in1=acts[(cell, j, 2)][:], op=ALU.mult)
+
+        def add_c(j, cell):
+            nc.vector.tensor_tensor(out=c_st[:, j, :], in0=acts[(cell, j, 1)][:], in1=acts[(cell, j, 0)][:], op=ALU.add)
+
+        def tanh_c(j, cell):
+            nc.scalar.activation(out=acts[(cell, j, 2)][:], in_=c_st[:, j, :], func=ACT.Tanh)
+
+        h2_tiles = {}
+
+        def mul_h(j, cell):
+            ao, th = acts[(cell, j, 3)], acts[(cell, j, 2)]
             if cell == 0:
-                nc.vector.tensor_tensor(out=h1_pl[:, j // 4, j % 4, :], in0=ao[:], in1=ag[:], op=ALU.mult)
-                return None
-            h2 = h2p.tile([P, NB], F32, tag="h2")
-            nc.vector.tensor_tensor(out=h2[:], in0=ao[:], in1=ag[:], op=ALU.mult)
-            return h2
+                nc.vector.tensor_tensor(out=h1_pl[:, j // 4, j % 4, :], in0=ao[:], in1=th[:], op=ALU.mult)
+            else:
+                h2 = h2p.tile([P, NB], F32, tag="h2")
+                nc.vector.tensor_tensor(out=h2[:], in0=ao[:], in1=th[:], op=ALU.mult)
+                h2_tiles[j] = h2
 
         def h1_quant(g):
-            nc.vector.tensor_copy(out=h1_grp[:, g], in_=h1_pl[:, g].rearrange("p t n -> p n t"))
             for n0, n1 in N_SPLIT:
+                nc.vector.tensor_copy(out=h1_grp[:, g, n0:n1, :], in_=h1_pl[:, g, :, n0:n1].rearrange("p t n -> p n t"))
                 nc.vector.quantize_mx(
                     out=h1_codes[:, g * NB + n0 : g * NB + n1].bitcast(FP8X4),
                     scales=h1_scales[:, g * NB + n0 : g * NB + n1],
                     in_=h1_flat[:, 4 * (g * NB + n0) : 4 * (g * NB + n1)],
                 )
 
-        out_h = out_0.rearrange("(p t) h -> p t h", t=3)
-        out_c = out_1.rearrange("(p t) h -> p t h", t=3)
+        out_views = (out_1.rearrange("(p t) h -> p t h", t=3), out_0.rearrange("(p t) h -> p t h", t=3))
 
-        def outputs(b, h2_pair):
-            o_sb = iop.tile([P, 2, 3, 256], F32, tag="io")
-            o5 = o_sb[:].rearrange("p w t (m e) -> p w t m e", e=2)
-            for t in range(3):
-                ot = psum_t.tile([P, 2, 2, P], F32, tag="tp")
+        def outputs(b):
+            for w in range(2):
+                o_sb = outp.tile([P, 3, 256], F32, tag="o")
+                o5 = o_sb[:].rearrange("p t (m e) -> p t m e", e=2)
+                two = psum.tile([P, 2, 2, P], F32, tag="bank")
+                one = psum.tile([P, 2, 2, P], F32, tag="bank")
                 for e in range(2):
-                    nc.tensor.transpose(ot[:, 0, e, :], c_st[:, 2 * b + e, 128 * t : 128 * t + 128], ident[:])
-                    nc.tensor.transpose(ot[:, 1, e, :], h2_pair[e][:, 128 * t : 128 * t + 128], ident[:])
-                nc.vector.tensor_copy(out=o5[:, :, t], in_=ot[:].rearrange("p w e m -> p w m e"))
-            nc.sync.dma_start(out=out_c[:, :, 256 * b : 256 * b + 256], in_=o_sb[:, 0])
-            nc.sync.dma_start(out=out_h[:, :, 256 * b : 256 * b + 256], in_=o_sb[:, 1])
+                    src = c_st[:, 2 * b + e, :] if w == 0 else h2_tiles[2 * b + e][:]
+                    for t in range(3):
+                        dst = two[:, t, e, :] if t < 2 else one[:, 0, e, :]
+                        nc.tensor.transpose(dst, src[:, 128 * t : 128 * t + 128], ident[:])
+                nc.vector.tensor_copy(out=o5[:, 0:2], in_=two[:].rearrange("p t e m -> p t m e"))
+                nc.scalar.copy(out=o5[:, 2:3], in_=one[:, 0:1].rearrange("p t e m -> p t m e"))
+                nc.sync.dma_start(out=out_views[w][:, :, 256 * b : 256 * b + 256], in_=o_sb[:])
 
-        weight_unit(0)
-        c0_prep()
-        for j in range(UNITS):
-            if j + 1 < UNITS:
-                weight_unit(j + 1)
-            epilogue(j, 0, gates_mx(j, 0))
-            if j == 3:
-                h1_quant(0)
+        evac_quantise(0, transposes(0), None)
+        for hh in range(HALVES):
+            j, hf = divmod(hh, 2)
+            banks = transposes(hh + 1) if hh + 1 < HALVES else None
+            if hh + RAW_BUFS < HALVES:
+                load_half(hh + RAW_BUFS)
+            prev = j - 1 if hf == 0 and j > 0 else None
+            if prev is not None:
+                mul_ig(prev, 0)
+                add_c(prev, 0)
+            if banks is not None:
+                evac_quantise(hh + 1, banks, (lambda: tanh_c(prev, 0)) if prev is not None else None)
+            if prev is not None:
+                mul_h(prev, 0)
+                if prev == 3:
+                    h1_quant(0)
+            if hh == 1:
+                c0_prep()
+            if hf == 1:
+                mul_fc(j, 0)
+            gate_mx(j, 2 * hf, 0)
+            gate_mx(j, 2 * hf + 1, 0)
+            gate_act(j, 2 * hf, 0)
+            gate_act(j, 2 * hf + 1, 0)
+        mul_ig(UNITS - 1, 0)
+        add_c(UNITS - 1, 0)
+        tanh_c(UNITS - 1, 0)
+        mul_h(UNITS - 1, 0)
         h1_quant(1)
-        pair = []
-        for j in range(UNITS):
-            pair.append(epilogue(j, 1, gates_mx(j, 1)))
-            if j % 2 == 1:
-                outputs(j // 2, pair)
-                pair = []
+
+        early = [(j, gi) for j in range(PRE_UNITS) for gi in range(4)]
+        for j, gi in early:
+            gt = psum.tile([P, NB], F32, tag="bank")
+            gates[(1, j, gi)] = gt
+            passes(gt, j, gi, 1, 0, (0, 1))
+        for j, gi in early:
+            passes(gates[(1, j, gi)], j, gi, 1, 0, (2,))
+        for j, gi in early:
+            passes(gates[(1, j, gi)], j, gi, 1, 1, (0, 1, 2))
+        for j in range(UNITS + OUT_DELAY):
+            if PRE_UNITS <= j < UNITS:
+                for gi in range(4):
+                    gate_mx(j, gi, 1)
+            if j < UNITS:
+                gate_act(j, 0, 1)
+            if 0 < j <= UNITS:
+                tanh_c(j - 1, 1)
+                mul_h(j - 1, 1)
+            if j < UNITS:
+                gate_act(j, 1, 1)
+                mul_fc(j, 1)
+                gate_act(j, 2, 1)
+                mul_ig(j, 1)
+                add_c(j, 1)
+                gate_act(j, 3, 1)
+            if j >= OUT_DELAY and (j - OUT_DELAY) % 2 == 1:
+                outputs((j - OUT_DELAY) // 2)

@@ -13,13 +13,15 @@ ALU = mybir.AluOpType
 
 P = 128
 NB = 384
+NA = 256
 UNITS = 8
-HALVES = 2 * UNITS
+PAIRS = 4
+BLOCKS = 16
 FLOPS = 2 * 2 * 384 * 4096 * 1536
-N_SPLIT = ((0, 256), (256, 384))
 RAW_BUFS = 8
 OUT_DELAY = 2
 PRE_UNITS = 2
+GATE_ORDER = (1, 0, 2, 3)
 GATE_FUNC = (ACT.Sigmoid, ACT.Sigmoid, ACT.Tanh, ACT.Sigmoid)
 
 
@@ -49,101 +51,142 @@ def tile_odelstmcell_pa_kernel(tc, inputs, h0, c0, w_ih, w_hh, b_ih, b_hh, out_0
         bias_raw = const.tile([P, 256], BF16)
         nc.vector.memset(bias_raw[:], 0.0)
 
-        x_raw = const.tile([P, 3 * 512], BF16)
-        nc.sync.dma_start(out=x_raw[:], in_=inputs.rearrange("(p t) k -> p (t k)", t=3))
-        h0_raw = const.tile([P, 3 * 1024], BF16)
-        nc.sync.dma_start(out=h0_raw[:], in_=h0.rearrange("(p t) k -> p (t k)", t=3))
-        nc.scalar.dma_start(out=bias_raw[0:16, :], in_=b_ih.rearrange("(r c) -> r c", c=256))
-        nc.scalar.dma_start(out=bias_raw[16:32, :], in_=b_hh.rearrange("(r c) -> r c", c=256))
-        c0_raw = const.tile([P, 3 * 1024], BF16)
-        wih_v = w_ih.rearrange("(g b p e) k -> b e p g k", g=4, b=4, p=P, e=2)
-        whh_v = w_hh.rearrange("(g b p e) k -> b e p g k", g=4, b=4, p=P, e=2)
+        def rows_a(x):
+            return x[0:NA, :].rearrange("(p t) k -> p t k", t=2)
+
+        def rows_b(x):
+            return x[NA:NB, :]
+
+        xa_raw = const.tile([P, 2, 512], BF16)
+        ha_raw = const.tile([P, 2, 1024], BF16)
+        ca_raw = const.tile([P, 2, 1024], BF16)
+        xb_raw = const.tile([P, 512], BF16)
+        hb_raw = const.tile([P, 1024], BF16)
+        cb_raw = const.tile([P, 1024], BF16)
+        wih_v = w_ih.rearrange("(g b p e) k -> b g p (e k)", g=4, b=4, p=P, e=2)
+        whh_v = w_hh.rearrange("(g b p e) k -> b g p (e k)", g=4, b=4, p=P, e=2)
         raw_views = {}
 
-        def load_half(hh):
-            j, hf = divmod(hh, 2)
-            b, e = divmod(j, 2)
+        def load_block(q):
+            b, o = divmod(q, 4)
+            gi = GATE_ORDER[o]
             wih_raw = rawp.tile([P, 2 * 512], BF16, tag="wih")
-            nc.sync.dma_start(
-                out=wih_raw[:].rearrange("p (g k) -> p g k", g=2), in_=wih_v[b, e][:, 2 * hf : 2 * hf + 2, :]
-            )
+            nc.sync.dma_start(out=wih_raw[:], in_=wih_v[b, gi])
             whh_raw = rawp.tile([P, 2 * 1024], BF16, tag="whh")
-            nc.sync.dma_start(
-                out=whh_raw[:].rearrange("p (g k) -> p g k", g=2), in_=whh_v[b, e][:, 2 * hf : 2 * hf + 2, :]
-            )
-            raw_views[hh] = (
-                wih_raw[:].bitcast(F32).rearrange("p (g w) -> p g w", g=2),
-                whh_raw[:].bitcast(F32).rearrange("p (g w) -> p g w", g=2),
+            nc.sync.dma_start(out=whh_raw[:], in_=whh_v[b, gi])
+            raw_views[q] = (
+                wih_raw[:].bitcast(F32).rearrange("p (e w) -> p e w", e=2),
+                whh_raw[:].bitcast(F32).rearrange("p (e w) -> p e w", e=2),
             )
 
-        for hh in range(RAW_BUFS):
-            load_half(hh)
-            if hh == 2:
-                nc.sync.dma_start(out=c0_raw[:], in_=c0.rearrange("(p t) k -> p (t k)", t=3))
-        x_f = x_raw[:].bitcast(F32).rearrange("p (t w) -> p t w", t=3)
-        h0_f = h0_raw[:].bitcast(F32).rearrange("p (t w) -> p t w", t=3)
-        c0_f = c0_raw[:].bitcast(F32).rearrange("p (t w) -> p t w", t=3)
+        nc.sync.dma_start(out=xa_raw[:], in_=rows_a(inputs))
+        nc.sync.dma_start(out=ha_raw[:], in_=rows_a(h0))
+        nc.scalar.dma_start(out=bias_raw[0:16, :], in_=b_ih.rearrange("(r c) -> r c", c=256))
+        nc.scalar.dma_start(out=bias_raw[16:32, :], in_=b_hh.rearrange("(r c) -> r c", c=256))
+        for q in range(RAW_BUFS):
+            load_block(q)
+            if q == 1:
+                nc.sync.dma_start(out=ca_raw[:], in_=rows_a(c0))
+        nc.sync.dma_start(out=xb_raw[:], in_=rows_b(inputs))
+        nc.sync.dma_start(out=hb_raw[:], in_=rows_b(h0))
+        nc.sync.dma_start(out=cb_raw[:], in_=rows_b(c0))
+        xa_f = xa_raw[:].rearrange("p t k -> p (t k)").bitcast(F32).rearrange("p (t w) -> p t w", t=2)
+        ha_f = ha_raw[:].rearrange("p t k -> p (t k)").bitcast(F32).rearrange("p (t w) -> p t w", t=2)
+        ca_f = ca_raw[:].rearrange("p t k -> p (t k)").bitcast(F32).rearrange("p (t w) -> p t w", t=2)
+        xb_f = xb_raw[:].bitcast(F32)
+        hb_f = hb_raw[:].bitcast(F32)
+        cb_f = cb_raw[:].bitcast(F32)
 
-        a_grp = const.tile([P, 3 * NB * 2], F32, align_bytes=64)
-        a_grp5 = a_grp[:].rearrange("p (s t m u) -> p s t m u", s=3, t=3, u=2)
-        a_bf = a_grp[:].bitcast(BF16)
-        a_codes = const.tile([P, 3 * NB], U32, align_bytes=64)
-        a_scales = const.tile([P, 3 * NB], U8, align_bytes=64)
+        aA_grp = const.tile([P, 3 * NA * 2], F32, align_bytes=64)
+        aB_grp = const.tile([P, 3 * P * 2], F32, align_bytes=64)
+        aA_codes = const.tile([P, 3 * NA], U32, align_bytes=64)
+        aA_scales = const.tile([P, 3 * NA], U8, align_bytes=64)
+        aB_codes = const.tile([P, 3 * P], U32, align_bytes=64)
+        aB_scales = const.tile([P, 3 * P], U8, align_bytes=64)
         h1_pl = const.tile([P, 2, 4, NB], BF16)
-        h1_grp = const.tile([P, 2, NB, 4], BF16, align_bytes=64)
-        h1_flat = h1_grp[:].rearrange("p g n t -> p (g n t)")
-        h1_codes = const.tile([P, 2 * NB], U32, align_bytes=64)
-        h1_scales = const.tile([P, 2 * NB], U8, align_bytes=64)
-        c0T = const.tile([P, 4 * NB], F32)
-        c0T_bf = c0T[:].bitcast(BF16).rearrange("p (b n e) -> p b n e", b=4, e=2)
+        hA_grp = const.tile([P, 2, NA, 4], BF16, align_bytes=64)
+        hB_grp = const.tile([P, 2, P, 4], BF16, align_bytes=64)
+        hA_codes = const.tile([P, 2 * NA], U32, align_bytes=64)
+        hA_scales = const.tile([P, 2 * NA], U8, align_bytes=64)
+        hB_codes = const.tile([P, 2 * P], U32, align_bytes=64)
+        hB_scales = const.tile([P, 2 * P], U8, align_bytes=64)
+        c0T = const.tile([P, PAIRS * NB], F32)
+        c0T_w = c0T[:].rearrange("p (b n) -> p b n", b=PAIRS)
+        c0T_bf = c0T[:].bitcast(BF16).rearrange("p (b n e) -> p b e n", b=PAIRS, e=2)
         c_st = const.tile([P, UNITS, NB], F32)
         w_codes = const.tile([P, 96 * P], U32, align_bytes=64)
         w_scales = const.tile([P, 96 * P], U8, align_bytes=64)
         bias_w = const.tile([P, 32], F32)
         bias = const.tile([P, 32], F32)
 
+        def quantise(codes, scales, grp_bf, lo, hi):
+            nc.vector.quantize_mx(
+                out=codes[:, lo:hi].bitcast(FP8X4), scales=scales[:, lo:hi], in_=grp_bf[:, 4 * lo : 4 * hi]
+            )
+
+        aA_grp5 = aA_grp[:].rearrange("p (s t m u) -> p s t m u", s=3, t=2, u=2)
         for s in range(3):
-            for t0, nt in ((0, 2), (2, 1)):
+            tp = psum.tile([P, 2, 2, P], F32, tag="bank")
+            for t in range(2):
+                for u in range(2):
+                    if s == 0:
+                        src = xa_f[:, t, 128 * u : 128 * u + 128]
+                    else:
+                        lo = 256 * (s - 1) + 128 * u
+                        src = ha_f[:, t, lo : lo + 128]
+                    nc.tensor.transpose(tp[:, t, u, :], src, ident[:])
+            evac("VSS"[s], aA_grp5[:, s], tp[:].rearrange("p t u m -> p t m u"))
+        for s in range(3):
+            quantise(aA_codes, aA_scales, aA_grp[:].bitcast(BF16), s * NA, (s + 1) * NA)
+
+        def bias_prep():
+            tp = psum.tile([P, 2, 2, P], F32, tag="bank")
+            nc.tensor.transpose(tp[:, 0, 0, :], bias_raw[:].bitcast(F32), ident[:])
+            nc.vector.tensor_copy(out=bias_w[:], in_=tp[:, 0, 0, 0:32])
+            bias_wb = bias_w[:].bitcast(BF16)
+            nc.vector.tensor_tensor(out=bias[:], in0=bias_wb[:, 0:32], in1=bias_wb[:, 32:64], op=ALU.add)
+
+        def acts_b_prep():
+            aB_grp4 = aB_grp[:].rearrange("p (s m u) -> p s m u", s=3, u=2)
+            for s0, ns in ((0, 2), (2, 1)):
                 tp = psum.tile([P, 2, 2, P], F32, tag="bank")
-                for tl in range(nt):
+                for sl in range(ns):
+                    s = s0 + sl
                     for u in range(2):
-                        if s == 0:
-                            src = x_f[:, t0 + tl, 128 * u : 128 * u + 128]
-                        else:
-                            lo = 256 * (s - 1) + 128 * u
-                            src = h0_f[:, t0 + tl, lo : lo + 128]
-                        nc.tensor.transpose(tp[:, tl, u, :], src, ident[:])
-                evac(
-                    "V" if nt == 2 else "S",
-                    a_grp5[:, s, t0 : t0 + nt],
-                    tp[:, 0:nt].rearrange("p t u m -> p t m u"),
-                )
-            for n0, n1 in N_SPLIT:
-                nc.vector.quantize_mx(
-                    out=a_codes[:, s * NB + n0 : s * NB + n1].bitcast(FP8X4),
-                    scales=a_scales[:, s * NB + n0 : s * NB + n1],
-                    in_=a_bf[:, 4 * (s * NB + n0) : 4 * (s * NB + n1)],
-                )
+                        lo = 256 * (s - 1) + 128 * u
+                        src = xb_f[:, 128 * u : 128 * u + 128] if s == 0 else hb_f[:, lo : lo + 128]
+                        nc.tensor.transpose(tp[:, sl, u, :], src, ident[:])
+                evac("VS"[s0 // 2], aB_grp4[:, s0 : s0 + ns], tp[:, 0:ns].rearrange("p s u m -> p s m u"))
+            quantise(aB_codes, aB_scales, aB_grp[:].bitcast(BF16), 0, 2 * P)
+            quantise(aB_codes, aB_scales, aB_grp[:].bitcast(BF16), 2 * P, 3 * P)
 
-        tp = psum.tile([P, 2, 2, P], F32, tag="bank")
-        nc.tensor.transpose(tp[:, 0, 0, :], bias_raw[:].bitcast(F32), ident[:])
-        nc.vector.tensor_copy(out=bias_w[:], in_=tp[:, 0, 0, 0:32])
-        bias_wb = bias_w[:].bitcast(BF16)
-        nc.vector.tensor_tensor(out=bias[:], in0=bias_wb[:, 0:32], in1=bias_wb[:, 32:64], op=ALU.add)
+        def c0_prep_a():
+            for b0 in (0, 2):
+                tp = psum.tile([P, 2, 2, P], F32, tag="bank")
+                for bl in range(2):
+                    for t in range(2):
+                        nc.tensor.transpose(tp[:, bl, t, :], ca_f[:, t, 128 * (b0 + bl) : 128 * (b0 + bl) + 128], ident[:])
+                evac("SV"[b0 // 2], c0T_w[:, b0 : b0 + 2, 0:NA], tp[:].rearrange("p b t m -> p b (t m)"))
 
-        def transposes(hh):
-            wih_f, whh_f = raw_views[hh]
+        def c0_prep_b():
+            tp = psum.tile([P, 4, P], F32, tag="bank")
+            for b in range(PAIRS):
+                nc.tensor.transpose(tp[:, b, :], cb_f[:, 128 * b : 128 * b + 128], ident[:])
+            evac("S", c0T_w[:, :, NA:NB], tp[:])
+
+        def transposes(q):
+            wih_f, whh_f = raw_views[q]
             banks = []
             for k in range(3):
                 tp = psum.tile([P, 2, 2, P], F32, tag="bank")
                 for i in range(2):
-                    gl, s = divmod(2 * k + i, 3)
+                    e, s = divmod(2 * k + i, 3)
                     for u in range(2):
                         if s == 0:
-                            src = wih_f[:, gl, 128 * u : 128 * u + 128]
+                            src = wih_f[:, e, 128 * u : 128 * u + 128]
                         else:
                             lo = 256 * (s - 1) + 128 * u
-                            src = whh_f[:, gl, lo : lo + 128]
+                            src = whh_f[:, e, lo : lo + 128]
                         nc.tensor.transpose(tp[:, i, u, :], src, ident[:])
                 banks.append(tp)
             return banks
@@ -153,174 +196,218 @@ def tile_odelstmcell_pa_kernel(tc, inputs, h0, c0, w_ih, w_hh, b_ih, b_hh, out_0
             evac(who, grp[:].rearrange("p (i m u) -> p i m u", i=2, u=2), bank[:].rearrange("p i u m -> p i m u"))
             return grp
 
-        def quantise_bank(hh, k, grp):
-            base = (hh * 6 + 2 * k) * P
+        def quantise_bank(q, k, grp):
+            base = (q * 6 + 2 * k) * P
             nc.vector.quantize_mx(
                 out=w_codes[:, base : base + 2 * P].bitcast(FP8X4),
                 scales=w_scales[:, base : base + 2 * P],
                 in_=grp[:].bitcast(BF16),
             )
 
-        def evac_quantise(hh, banks, between):
-            g0 = evac_bank("S", banks[0])
-            g1 = evac_bank("V", banks[1])
-            if between is not None:
-                between()
-            quantise_bank(hh, 0, g0)
-            quantise_bank(hh, 1, g1)
-            g2 = evac_bank("S", banks[2])
-            quantise_bank(hh, 2, g2)
-
-        def c0_prep():
-            for b in range(4):
-                tp = psum.tile([P, 512], F32, tag="bank")
-                for t in range(3):
-                    nc.tensor.transpose(tp[:, 128 * t : 128 * t + 128], c0_f[:, t, 128 * b : 128 * b + 128], ident[:])
-                evac("SV"[b % 2], c0T[:, NB * b : NB * b + NB], tp[:, 0:NB])
-
-        def passes(gt, j, gi, cell, part, which):
-            n0, n1 = N_SPLIT[part]
+        def passes(out, j, gi, cell, part, which=(0, 1, 2)):
+            b, e = divmod(j, 2)
+            q = 4 * b + GATE_ORDER.index(gi)
+            n = (NA, P)[part]
             for s in which:
-                col = (j * 12 + gi * 3 + s) * P
+                col = (q * 6 + e * 3 + s) * P
                 if s == 0 or cell == 0:
-                    rc, rs, off = a_codes, a_scales, s * NB
+                    rc, rs, off = (aA_codes, aB_codes)[part], (aA_scales, aB_scales)[part], s * n
                 else:
-                    rc, rs, off = h1_codes, h1_scales, (s - 1) * NB
+                    rc, rs, off = (hA_codes, hB_codes)[part], (hA_scales, hB_scales)[part], (s - 1) * n
                 nc.tensor.matmul_mx(
-                    out=gt[:, n0:n1],
+                    out=out,
                     lhsT=w_codes[:, col : col + P].bitcast(FP8X4),
                     lhsT_scale=w_scales[:, col : col + P],
-                    rhs=rc[:, off + n0 : off + n1].bitcast(FP8X4),
-                    rhs_scale=rs[:, off + n0 : off + n1],
+                    rhs=rc[:, off : off + n].bitcast(FP8X4),
+                    rhs_scale=rs[:, off : off + n],
                     start=(s == 0),
                     stop=(s == 2),
                 )
 
+        def act(out, in_, gi, j):
+            nc.scalar.activation(
+                out=out, in_=in_, func=GATE_FUNC[gi], bias=bias[:, 8 * gi + j : 8 * gi + j + 1]
+            )
+
+        def mult(out, in0, in1):
+            nc.vector.tensor_tensor(out=out, in0=in0, in1=in1, op=ALU.mult)
+
+        pa = {}
+
+        def cols(part):
+            return slice(0, NA) if part == 0 else slice(NA, NB)
+
+        def pair_act(b, gi, part, banks):
+            a = gact.tile([P, 2, (NA, P)[part]], F32, tag="g%d" % gi)
+            for e in range(2):
+                act(a[:, e, :], banks[e], gi, 2 * b + e)
+            pa[(b, gi, part)] = a
+
+        def pair_fc(b, part):
+            a = pa[(b, 1, part)]
+            mult(a[:], a[:], c0T_bf[:, b, :, cols(part)])
+
+        def pair_ig(b, part):
+            a = pa[(b, 0, part)]
+            mult(a[:], a[:], pa[(b, 2, part)][:])
+
+        def pair_add(b, part):
+            nc.vector.tensor_tensor(
+                out=c_st[:, 2 * b : 2 * b + 2, cols(part)], in0=pa[(b, 1, part)][:], in1=pa[(b, 0, part)][:], op=ALU.add
+            )
+
+        def pair_tanh(b, part):
+            nc.scalar.activation(
+                out=pa[(b, 2, part)][:], in_=c_st[:, 2 * b : 2 * b + 2, cols(part)], func=ACT.Tanh
+            )
+
+        def pair_h(b, part):
+            t = 2 * (b % 2)
+            mult(h1_pl[:, b // 2, t : t + 2, cols(part)], pa[(b, 3, part)][:], pa[(b, 2, part)][:])
+
+        def h1_quant(g, part):
+            n = (NA, P)[part]
+            grp = (hA_grp, hB_grp)[part]
+            nc.vector.tensor_copy(out=grp[:, g], in_=h1_pl[:, g, :, cols(part)].rearrange("p t n -> p n t"))
+            quantise(
+                (hA_codes, hB_codes)[part],
+                (hA_scales, hB_scales)[part],
+                grp[:].rearrange("p g n t -> p (g n t)"),
+                g * n,
+                (g + 1) * n,
+            )
+
+        tb = transposes(0)
+        g0 = evac_bank("S", tb[0])
+        g1 = evac_bank("V", tb[1])
+        g2 = evac_bank("S", tb[2])
+        quantise_bank(0, 0, g0)
+        quantise_bank(0, 1, g1)
+        quantise_bank(0, 2, g2)
+        bias_prep()
+        for q in range(BLOCKS):
+            b, o = divmod(q, 4)
+            gi = GATE_ORDER[o]
+            more = q + 1 < BLOCKS
+            if more:
+                tb = transposes(q + 1)
+                if q + RAW_BUFS < BLOCKS:
+                    load_block(q + RAW_BUFS)
+                g0 = evac_bank("S", tb[0])
+                g1 = evac_bank("V", tb[1])
+            if o == 0 and b > 0:
+                pair_add(b - 1, 0)
+            if o == 1 and b > 0:
+                pair_h(b - 1, 0)
+            if o == 2:
+                pair_fc(b, 0)
+            if o == 3:
+                pair_ig(b, 0)
+            if more:
+                g2 = evac_bank("S", tb[2])
+            if o == 0 and b > 0:
+                pair_tanh(b - 1, 0)
+            if more:
+                quantise_bank(q + 1, 0, g0)
+                quantise_bank(q + 1, 1, g1)
+                quantise_bank(q + 1, 2, g2)
+            if q == 1:
+                c0_prep_a()
+            if q == 10:
+                h1_quant(0, 0)
+            gt = psum.tile([P, 2, NA], F32, tag="bank")
+            for e in range(2):
+                passes(gt[:, e, :], 2 * b + e, gi, 0, 0)
+            pair_act(b, gi, 0, [gt[:, e, :] for e in range(2)])
+            if q == 11:
+                acts_b_prep()
+            if q == 12:
+                c0_prep_b()
+        pair_add(PAIRS - 1, 0)
+        pair_tanh(PAIRS - 1, 0)
+
+        for b in range(PAIRS):
+            fi = psum.tile([P, 4, P], F32, tag="bank")
+            go = psum.tile([P, 4, P], F32, tag="bank")
+            for bank, gates2 in ((fi, (1, 0)), (go, (2, 3))):
+                for l in range(2):
+                    for e in range(2):
+                        passes(bank[:, 2 * l + e, :], 2 * b + e, gates2[l], 0, 1)
+            if b == 0:
+                pair_h(PAIRS - 1, 0)
+                h1_quant(1, 0)
+            pair_act(b, 1, 1, [fi[:, e, :] for e in range(2)])
+            pair_act(b, 0, 1, [fi[:, 2 + e, :] for e in range(2)])
+            pair_fc(b, 1)
+            if b > 0:
+                pair_tanh(b - 1, 1)
+                pair_h(b - 1, 1)
+                if b == 2:
+                    h1_quant(0, 1)
+            pair_act(b, 2, 1, [go[:, e, :] for e in range(2)])
+            pair_ig(b, 1)
+            pair_add(b, 1)
+            pair_act(b, 3, 1, [go[:, 2 + e, :] for e in range(2)])
+        pair_tanh(PAIRS - 1, 1)
+        pair_h(PAIRS - 1, 1)
+        h1_quant(1, 1)
+
         gates = {}
         acts = {}
-
-        def gate_mx(j, gi, cell):
-            gt = psum.tile([P, NB], F32, tag="bank")
-            passes(gt, j, gi, cell, 0, (0, 1, 2))
-            passes(gt, j, gi, cell, 1, (0, 1, 2))
-            gates[(cell, j, gi)] = gt
-
-        def gate_act(j, gi, cell):
-            a = gact.tile([P, NB], F32, tag="a%d" % gi)
-            nc.scalar.activation(
-                out=a[:],
-                in_=gates[(cell, j, gi)][:],
-                func=GATE_FUNC[gi],
-                bias=bias[:, 8 * gi + j : 8 * gi + j + 1],
-            )
-            acts[(cell, j, gi)] = a
-
-        def mul_fc(j, cell):
-            af = acts[(cell, j, 1)]
-            cprev = c0T_bf[:, j // 2, :, j % 2] if cell == 0 else c_st[:, j, :]
-            nc.vector.tensor_tensor(out=af[:], in0=af[:], in1=cprev, op=ALU.mult)
-
-        def mul_ig(j, cell):
-            ai = acts[(cell, j, 0)]
-            nc.vector.tensor_tensor(out=ai[:], in0=ai[:], in1=acts[(cell, j, 2)][:], op=ALU.mult)
-
-        def add_c(j, cell):
-            nc.vector.tensor_tensor(out=c_st[:, j, :], in0=acts[(cell, j, 1)][:], in1=acts[(cell, j, 0)][:], op=ALU.add)
-
-        def tanh_c(j, cell):
-            nc.scalar.activation(out=acts[(cell, j, 2)][:], in_=c_st[:, j, :], func=ACT.Tanh)
-
         h2_tiles = {}
 
-        def mul_h(j, cell):
-            ao, th = acts[(cell, j, 3)], acts[(cell, j, 2)]
-            if cell == 0:
-                nc.vector.tensor_tensor(out=h1_pl[:, j // 4, j % 4, :], in0=ao[:], in1=th[:], op=ALU.mult)
-            else:
-                h2 = h2p.tile([P, NB], F32, tag="h2")
-                nc.vector.tensor_tensor(out=h2[:], in0=ao[:], in1=th[:], op=ALU.mult)
-                h2_tiles[j] = h2
+        def gate_act(j, gi):
+            a = gact.tile([P, NB], F32, tag="g%d" % gi)
+            act(a[:], gates[(j, gi)][:], gi, j)
+            acts[(j, gi)] = a
 
-        def h1_quant(g):
-            for n0, n1 in N_SPLIT:
-                nc.vector.tensor_copy(out=h1_grp[:, g, n0:n1, :], in_=h1_pl[:, g, :, n0:n1].rearrange("p t n -> p n t"))
-                nc.vector.quantize_mx(
-                    out=h1_codes[:, g * NB + n0 : g * NB + n1].bitcast(FP8X4),
-                    scales=h1_scales[:, g * NB + n0 : g * NB + n1],
-                    in_=h1_flat[:, 4 * (g * NB + n0) : 4 * (g * NB + n1)],
-                )
-
-        out_views = (out_1.rearrange("(p t) h -> p t h", t=3), out_0.rearrange("(p t) h -> p t h", t=3))
-
-        def outputs(b):
-            for w in range(2):
-                o_sb = outp.tile([P, 3, 256], F32, tag="o")
-                o5 = o_sb[:].rearrange("p t (m e) -> p t m e", e=2)
+        def out_pair(b):
+            for w, dram in ((0, out_1), (1, out_0)):
+                oa = outp.tile([P, 2, 256], F32, tag="oa")
+                ob = outp.tile([P, 256], F32, tag="ob")
                 two = psum.tile([P, 2, 2, P], F32, tag="bank")
-                one = psum.tile([P, 2, 2, P], F32, tag="bank")
+                one = psum.tile([P, 2, P], F32, tag="bank")
                 for e in range(2):
                     src = c_st[:, 2 * b + e, :] if w == 0 else h2_tiles[2 * b + e][:]
                     for t in range(3):
-                        dst = two[:, t, e, :] if t < 2 else one[:, 0, e, :]
+                        dst = two[:, t, e, :] if t < 2 else one[:, e, :]
                         nc.tensor.transpose(dst, src[:, 128 * t : 128 * t + 128], ident[:])
-                nc.vector.tensor_copy(out=o5[:, 0:2], in_=two[:].rearrange("p t e m -> p t m e"))
-                nc.scalar.copy(out=o5[:, 2:3], in_=one[:, 0:1].rearrange("p t e m -> p t m e"))
-                nc.sync.dma_start(out=out_views[w][:, :, 256 * b : 256 * b + 256], in_=o_sb[:])
-
-        evac_quantise(0, transposes(0), None)
-        for hh in range(HALVES):
-            j, hf = divmod(hh, 2)
-            banks = transposes(hh + 1) if hh + 1 < HALVES else None
-            if hh + RAW_BUFS < HALVES:
-                load_half(hh + RAW_BUFS)
-            prev = j - 1 if hf == 0 and j > 0 else None
-            if prev is not None:
-                mul_ig(prev, 0)
-                add_c(prev, 0)
-            if banks is not None:
-                evac_quantise(hh + 1, banks, (lambda: tanh_c(prev, 0)) if prev is not None else None)
-            if prev is not None:
-                mul_h(prev, 0)
-                if prev == 3:
-                    h1_quant(0)
-            if hh == 1:
-                c0_prep()
-            if hf == 1:
-                mul_fc(j, 0)
-            gate_mx(j, 2 * hf, 0)
-            gate_mx(j, 2 * hf + 1, 0)
-            gate_act(j, 2 * hf, 0)
-            gate_act(j, 2 * hf + 1, 0)
-        mul_ig(UNITS - 1, 0)
-        add_c(UNITS - 1, 0)
-        tanh_c(UNITS - 1, 0)
-        mul_h(UNITS - 1, 0)
-        h1_quant(1)
+                nc.vector.tensor_copy(
+                    out=oa[:].rearrange("p t (m e) -> p t m e", e=2), in_=two[:].rearrange("p t e m -> p t m e")
+                )
+                nc.scalar.copy(out=ob[:].rearrange("p (m e) -> p m e", e=2), in_=one[:].rearrange("p e m -> p m e"))
+                nc.sync.dma_start(out=rows_a(dram)[:, :, 256 * b : 256 * b + 256], in_=oa[:])
+                nc.sync.dma_start(out=rows_b(dram)[:, 256 * b : 256 * b + 256], in_=ob[:])
 
         early = [(j, gi) for j in range(PRE_UNITS) for gi in range(4)]
         for j, gi in early:
             gt = psum.tile([P, NB], F32, tag="bank")
-            gates[(1, j, gi)] = gt
-            passes(gt, j, gi, 1, 0, (0, 1))
+            gates[(j, gi)] = gt
+            passes(gt[:, 0:NA], j, gi, 1, 0)
         for j, gi in early:
-            passes(gates[(1, j, gi)], j, gi, 1, 0, (2,))
-        for j, gi in early:
-            passes(gates[(1, j, gi)], j, gi, 1, 1, (0, 1, 2))
+            passes(gates[(j, gi)][:, NA:NB], j, gi, 1, 1)
         for j in range(UNITS + OUT_DELAY):
             if PRE_UNITS <= j < UNITS:
                 for gi in range(4):
-                    gate_mx(j, gi, 1)
+                    gt = psum.tile([P, NB], F32, tag="bank")
+                    gates[(j, gi)] = gt
+                    for part in range(2):
+                        passes(gt[:, cols(part)], j, gi, 1, part)
             if j < UNITS:
-                gate_act(j, 0, 1)
+                gate_act(j, 0)
             if 0 < j <= UNITS:
-                tanh_c(j - 1, 1)
-                mul_h(j - 1, 1)
+                jp = j - 1
+                th = acts[(jp, 2)]
+                nc.scalar.activation(out=th[:], in_=c_st[:, jp, :], func=ACT.Tanh)
+                h2 = h2p.tile([P, NB], F32, tag="h2")
+                mult(h2[:], acts[(jp, 3)][:], th[:])
+                h2_tiles[jp] = h2
             if j < UNITS:
-                gate_act(j, 1, 1)
-                mul_fc(j, 1)
-                gate_act(j, 2, 1)
-                mul_ig(j, 1)
-                add_c(j, 1)
-                gate_act(j, 3, 1)
+                gate_act(j, 1)
+                mult(acts[(j, 1)][:], acts[(j, 1)][:], c_st[:, j, :])
+                gate_act(j, 2)
+                mult(acts[(j, 0)][:], acts[(j, 0)][:], acts[(j, 2)][:])
+                nc.vector.tensor_tensor(out=c_st[:, j, :], in0=acts[(j, 1)][:], in1=acts[(j, 0)][:], op=ALU.add)
+                gate_act(j, 3)
             if j >= OUT_DELAY and (j - OUT_DELAY) % 2 == 1:
-                outputs((j - OUT_DELAY) // 2)
+                out_pair((j - OUT_DELAY) // 2)

@@ -20,7 +20,6 @@ BLOCKS = 16
 FLOPS = 2 * 2 * 384 * 4096 * 1536
 RAW_BUFS = 8
 OUT_DELAY = 2
-PRE_UNITS = 2
 GATE_ORDER = (1, 0, 2, 3)
 GATE_FUNC = (ACT.Sigmoid, ACT.Sigmoid, ACT.Tanh, ACT.Sigmoid)
 
@@ -30,10 +29,9 @@ def tile_odelstmcell_pa_kernel(tc, inputs, h0, c0, w_ih, w_hh, b_ih, b_hh, out_0
     with ExitStack() as ctx:
         const = ctx.enter_context(tc.tile_pool(name="const", bufs=1))
         rawp = ctx.enter_context(tc.tile_pool(name="rawp", bufs=RAW_BUFS))
-        grpp = ctx.enter_context(tc.tile_pool(name="grpp", bufs=6))
+        grpp = ctx.enter_context(tc.tile_pool(name="grpp", bufs=3))
         gact = ctx.enter_context(tc.tile_pool(name="gact", bufs=3))
-        h2p = ctx.enter_context(tc.tile_pool(name="h2p", bufs=4))
-        outp = ctx.enter_context(tc.tile_pool(name="outp", bufs=4))
+        outp = ctx.enter_context(tc.tile_pool(name="outp", bufs=2))
         psum = ctx.enter_context(tc.psum_pool(name="psum", bufs=8))
         ctx.enter_context(tc.manual_schedule())
 
@@ -110,9 +108,8 @@ def tile_odelstmcell_pa_kernel(tc, inputs, h0, c0, w_ih, w_hh, b_ih, b_hh, out_0
         hA_scales = const.tile([P, 2 * NA], U8, align_bytes=64)
         hB_codes = const.tile([P, 2 * P], U32, align_bytes=64)
         hB_scales = const.tile([P, 2 * P], U8, align_bytes=64)
-        c0T = const.tile([P, PAIRS * NB], F32)
-        c0T_w = c0T[:].rearrange("p (b n) -> p b n", b=PAIRS)
-        c0T_bf = c0T[:].bitcast(BF16).rearrange("p (b n e) -> p b e n", b=PAIRS, e=2)
+        c0B = const.tile([P, PAIRS * P], F32)
+        c0B_bf = c0B[:].bitcast(BF16).rearrange("p (b n e) -> p b e n", b=PAIRS, e=2)
         c_st = const.tile([P, UNITS, NB], F32)
         w_codes = const.tile([P, 96 * P], U32, align_bytes=64)
         w_scales = const.tile([P, 96 * P], U8, align_bytes=64)
@@ -160,19 +157,19 @@ def tile_odelstmcell_pa_kernel(tc, inputs, h0, c0, w_ih, w_hh, b_ih, b_hh, out_0
             quantise(aB_codes, aB_scales, aB_grp[:].bitcast(BF16), 0, 2 * P)
             quantise(aB_codes, aB_scales, aB_grp[:].bitcast(BF16), 2 * P, 3 * P)
 
-        def c0_prep_a():
-            for b0 in (0, 2):
-                tp = psum.tile([P, 2, 2, P], F32, tag="bank")
-                for bl in range(2):
-                    for t in range(2):
-                        nc.tensor.transpose(tp[:, bl, t, :], ca_f[:, t, 128 * (b0 + bl) : 128 * (b0 + bl) + 128], ident[:])
-                evac("SV"[b0 // 2], c0T_w[:, b0 : b0 + 2, 0:NA], tp[:].rearrange("p b t m -> p b (t m)"))
+        c0_psum = {}
+
+        def c0_prep_a(b):
+            tp = psum.tile([P, NA], F32, tag="bank")
+            for t in range(2):
+                nc.tensor.transpose(tp[:, 128 * t : 128 * t + 128], ca_f[:, t, 128 * b : 128 * b + 128], ident[:])
+            c0_psum[b] = tp[:].bitcast(BF16).rearrange("p (n e) -> p e n", e=2)
 
         def c0_prep_b():
-            tp = psum.tile([P, 4, P], F32, tag="bank")
+            tp = psum.tile([P, PAIRS * P], F32, tag="bank")
             for b in range(PAIRS):
-                nc.tensor.transpose(tp[:, b, :], cb_f[:, 128 * b : 128 * b + 128], ident[:])
-            evac("S", c0T_w[:, :, NA:NB], tp[:])
+                nc.tensor.transpose(tp[:, 128 * b : 128 * b + 128], cb_f[:, 128 * b : 128 * b + 128], ident[:])
+            evac("S", c0B[:], tp[:])
 
         def transposes(q):
             wih_f, whh_f = raw_views[q]
@@ -191,18 +188,22 @@ def tile_odelstmcell_pa_kernel(tc, inputs, h0, c0, w_ih, w_hh, b_ih, b_hh, out_0
                 banks.append(tp)
             return banks
 
-        def evac_bank(who, bank):
-            grp = grpp.tile([P, 512], F32, tag="grp", align_bytes=64)
-            evac(who, grp[:].rearrange("p (i m u) -> p i m u", i=2, u=2), bank[:].rearrange("p i u m -> p i m u"))
-            return grp
-
-        def quantise_bank(q, k, grp):
-            base = (q * 6 + 2 * k) * P
-            nc.vector.quantize_mx(
-                out=w_codes[:, base : base + 2 * P].bitcast(FP8X4),
-                scales=w_scales[:, base : base + 2 * P],
-                in_=grp[:].bitcast(BF16),
+        def evac_bank(who, grp, k, bank):
+            evac(
+                who,
+                grp[:, 512 * k : 512 * k + 512].rearrange("p (i m u) -> p i m u", i=2, u=2),
+                bank[:].rearrange("p i u m -> p i m u"),
             )
+
+        def quantise_block(q, grp):
+            grp_bf = grp[:].bitcast(BF16)
+            for lo, hi in ((0, 4 * P), (4 * P, 6 * P)):
+                base = q * 6 * P
+                nc.vector.quantize_mx(
+                    out=w_codes[:, base + lo : base + hi].bitcast(FP8X4),
+                    scales=w_scales[:, base + lo : base + hi],
+                    in_=grp_bf[:, 4 * lo : 4 * hi],
+                )
 
         def passes(out, j, gi, cell, part, which=(0, 1, 2)):
             b, e = divmod(j, 2)
@@ -243,9 +244,13 @@ def tile_odelstmcell_pa_kernel(tc, inputs, h0, c0, w_ih, w_hh, b_ih, b_hh, out_0
                 act(a[:, e, :], banks[e], gi, 2 * b + e)
             pa[(b, gi, part)] = a
 
-        def pair_fc(b, part):
+        def pair_fc(b, part, cell):
             a = pa[(b, 1, part)]
-            mult(a[:], a[:], c0T_bf[:, b, :, cols(part)])
+            if cell == 1:
+                c = c_st[:, 2 * b : 2 * b + 2, cols(part)]
+            else:
+                c = c0_psum[b] if part == 0 else c0B_bf[:, b]
+            mult(a[:], a[:], c)
 
         def pair_ig(b, part):
             a = pa[(b, 0, part)]
@@ -278,12 +283,10 @@ def tile_odelstmcell_pa_kernel(tc, inputs, h0, c0, w_ih, w_hh, b_ih, b_hh, out_0
             )
 
         tb = transposes(0)
-        g0 = evac_bank("S", tb[0])
-        g1 = evac_bank("V", tb[1])
-        g2 = evac_bank("S", tb[2])
-        quantise_bank(0, 0, g0)
-        quantise_bank(0, 1, g1)
-        quantise_bank(0, 2, g2)
+        grp = grpp.tile([P, 6 * 2 * P], F32, tag="grp", align_bytes=64)
+        for k in range(3):
+            evac_bank("SVS"[k], grp, k, tb[k])
+        quantise_block(0, grp)
         bias_prep()
         for q in range(BLOCKS):
             b, o = divmod(q, 4)
@@ -291,28 +294,28 @@ def tile_odelstmcell_pa_kernel(tc, inputs, h0, c0, w_ih, w_hh, b_ih, b_hh, out_0
             more = q + 1 < BLOCKS
             if more:
                 tb = transposes(q + 1)
+            if o == 1:
+                c0_prep_a(b)
+            if more:
                 if q + RAW_BUFS < BLOCKS:
                     load_block(q + RAW_BUFS)
-                g0 = evac_bank("S", tb[0])
-                g1 = evac_bank("V", tb[1])
+                grp = grpp.tile([P, 6 * 2 * P], F32, tag="grp", align_bytes=64)
+                evac_bank("S", grp, 0, tb[0])
+                evac_bank("V", grp, 1, tb[1])
             if o == 0 and b > 0:
                 pair_add(b - 1, 0)
             if o == 1 and b > 0:
                 pair_h(b - 1, 0)
             if o == 2:
-                pair_fc(b, 0)
+                pair_fc(b, 0, 0)
             if o == 3:
                 pair_ig(b, 0)
             if more:
-                g2 = evac_bank("S", tb[2])
+                evac_bank("S", grp, 2, tb[2])
             if o == 0 and b > 0:
                 pair_tanh(b - 1, 0)
             if more:
-                quantise_bank(q + 1, 0, g0)
-                quantise_bank(q + 1, 1, g1)
-                quantise_bank(q + 1, 2, g2)
-            if q == 1:
-                c0_prep_a()
+                quantise_block(q + 1, grp)
             if q == 10:
                 h1_quant(0, 0)
             gt = psum.tile([P, 2, NA], F32, tag="bank")
@@ -326,88 +329,80 @@ def tile_odelstmcell_pa_kernel(tc, inputs, h0, c0, w_ih, w_hh, b_ih, b_hh, out_0
         pair_add(PAIRS - 1, 0)
         pair_tanh(PAIRS - 1, 0)
 
-        for b in range(PAIRS):
-            fi = psum.tile([P, 4, P], F32, tag="bank")
-            go = psum.tile([P, 4, P], F32, tag="bank")
-            for bank, gates2 in ((fi, (1, 0)), (go, (2, 3))):
-                for l in range(2):
+        def gate_mx(b, part, cell):
+            n = (NA, P)[part]
+            out = {}
+            gates_per_bank = 512 // (2 * n)
+            for g0 in range(0, 4, gates_per_bank):
+                bank = psum.tile([P, 2 * gates_per_bank, n], F32, tag="bank")
+                for l in range(gates_per_bank):
+                    gi = GATE_ORDER[g0 + l]
                     for e in range(2):
-                        passes(bank[:, 2 * l + e, :], 2 * b + e, gates2[l], 0, 1)
+                        passes(bank[:, 2 * l + e, :], 2 * b + e, gi, cell, part)
+                    out[gi] = [bank[:, 2 * l + e, :] for e in range(2)]
+            return out
+
+        for b in range(PAIRS):
+            gt = gate_mx(b, 1, 0)
             if b == 0:
                 pair_h(PAIRS - 1, 0)
                 h1_quant(1, 0)
-            pair_act(b, 1, 1, [fi[:, e, :] for e in range(2)])
-            pair_act(b, 0, 1, [fi[:, 2 + e, :] for e in range(2)])
-            pair_fc(b, 1)
+            pair_act(b, 1, 1, gt[1])
+            pair_act(b, 0, 1, gt[0])
+            pair_fc(b, 1, 0)
             if b > 0:
                 pair_tanh(b - 1, 1)
                 pair_h(b - 1, 1)
                 if b == 2:
                     h1_quant(0, 1)
-            pair_act(b, 2, 1, [go[:, e, :] for e in range(2)])
+            pair_act(b, 2, 1, gt[2])
             pair_ig(b, 1)
             pair_add(b, 1)
-            pair_act(b, 3, 1, [go[:, 2 + e, :] for e in range(2)])
+            pair_act(b, 3, 1, gt[3])
         pair_tanh(PAIRS - 1, 1)
         pair_h(PAIRS - 1, 1)
         h1_quant(1, 1)
 
-        gates = {}
-        acts = {}
-        h2_tiles = {}
-
-        def gate_act(j, gi):
-            a = gact.tile([P, NB], F32, tag="g%d" % gi)
-            act(a[:], gates[(j, gi)][:], gi, j)
-            acts[(j, gi)] = a
-
-        def out_pair(b):
-            for w, dram in ((0, out_1), (1, out_0)):
-                oa = outp.tile([P, 2, 256], F32, tag="oa")
-                ob = outp.tile([P, 256], F32, tag="ob")
-                two = psum.tile([P, 2, 2, P], F32, tag="bank")
-                one = psum.tile([P, 2, P], F32, tag="bank")
+        def output(b, part):
+            nt = 2 - part
+            c_ps = psum.tile([P, nt, 2, P], F32, tag="bank")
+            o_ps = psum.tile([P, nt, 2, P], F32, tag="bank")
+            for t in range(nt):
                 for e in range(2):
-                    src = c_st[:, 2 * b + e, :] if w == 0 else h2_tiles[2 * b + e][:]
-                    for t in range(3):
-                        dst = two[:, t, e, :] if t < 2 else one[:, e, :]
-                        nc.tensor.transpose(dst, src[:, 128 * t : 128 * t + 128], ident[:])
-                nc.vector.tensor_copy(
-                    out=oa[:].rearrange("p t (m e) -> p t m e", e=2), in_=two[:].rearrange("p t e m -> p t m e")
-                )
-                nc.scalar.copy(out=ob[:].rearrange("p (m e) -> p m e", e=2), in_=one[:].rearrange("p e m -> p m e"))
-                nc.sync.dma_start(out=rows_a(dram)[:, :, 256 * b : 256 * b + 256], in_=oa[:])
-                nc.sync.dma_start(out=rows_b(dram)[:, 256 * b : 256 * b + 256], in_=ob[:])
+                    lo = NA * part + 128 * t
+                    nc.tensor.transpose(c_ps[:, t, e, :], c_st[:, 2 * b + e, lo : lo + 128], ident[:])
+            for t in range(nt):
+                for e in range(2):
+                    nc.tensor.transpose(o_ps[:, t, e, :], pa[(b, 3, part)][:, e, 128 * t : 128 * t + 128], ident[:])
+            c_sb = outp.tile([P, nt, 2 * P], F32, tag="c%d" % part)
+            h_sb = outp.tile([P, nt, 2 * P], F32, tag="h%d" % part)
+            th = outp.tile([P, nt, 2, P], F32, tag="t%d" % part)
+            nc.scalar.activation(out=th[:], in_=c_ps[:], func=ACT.Tanh)
+            nc.vector.tensor_copy(
+                out=c_sb[:].rearrange("p t (m e) -> p t m e", e=2), in_=c_ps[:].rearrange("p t e m -> p t m e")
+            )
+            mult(
+                h_sb[:].rearrange("p t (m e) -> p t m e", e=2),
+                o_ps[:].rearrange("p t e m -> p t m e"),
+                th[:].rearrange("p t e m -> p t m e"),
+            )
+            for dram, sb in ((out_1, c_sb), (out_0, h_sb)):
+                if part == 0:
+                    nc.sync.dma_start(out=rows_a(dram)[:, :, 256 * b : 256 * b + 256], in_=sb[:])
+                else:
+                    nc.sync.dma_start(out=rows_b(dram)[:, 256 * b : 256 * b + 256], in_=sb[:, 0, :])
 
-        early = [(j, gi) for j in range(PRE_UNITS) for gi in range(4)]
-        for j, gi in early:
-            gt = psum.tile([P, NB], F32, tag="bank")
-            gates[(j, gi)] = gt
-            passes(gt[:, 0:NA], j, gi, 1, 0)
-        for j, gi in early:
-            passes(gates[(j, gi)][:, NA:NB], j, gi, 1, 1)
-        for j in range(UNITS + OUT_DELAY):
-            if PRE_UNITS <= j < UNITS:
-                for gi in range(4):
-                    gt = psum.tile([P, NB], F32, tag="bank")
-                    gates[(j, gi)] = gt
-                    for part in range(2):
-                        passes(gt[:, cols(part)], j, gi, 1, part)
-            if j < UNITS:
-                gate_act(j, 0)
-            if 0 < j <= UNITS:
-                jp = j - 1
-                th = acts[(jp, 2)]
-                nc.scalar.activation(out=th[:], in_=c_st[:, jp, :], func=ACT.Tanh)
-                h2 = h2p.tile([P, NB], F32, tag="h2")
-                mult(h2[:], acts[(jp, 3)][:], th[:])
-                h2_tiles[jp] = h2
-            if j < UNITS:
-                gate_act(j, 1)
-                mult(acts[(j, 1)][:], acts[(j, 1)][:], c_st[:, j, :])
-                gate_act(j, 2)
-                mult(acts[(j, 0)][:], acts[(j, 0)][:], acts[(j, 2)][:])
-                nc.vector.tensor_tensor(out=c_st[:, j, :], in0=acts[(j, 1)][:], in1=acts[(j, 0)][:], op=ALU.add)
-                gate_act(j, 3)
-            if j >= OUT_DELAY and (j - OUT_DELAY) % 2 == 1:
-                out_pair((j - OUT_DELAY) // 2)
+        steps = [(b, part) for b0 in (0, 2) for part in range(2) for b in (b0, b0 + 1)]
+        for k in range(len(steps) + OUT_DELAY):
+            if k < len(steps):
+                b, part = steps[k]
+                gt = gate_mx(b, part, 1)
+                pair_act(b, 1, part, gt[1])
+                pair_fc(b, part, 1)
+                pair_act(b, 0, part, gt[0])
+                pair_act(b, 2, part, gt[2])
+                pair_ig(b, part)
+                pair_add(b, part)
+                pair_act(b, 3, part, gt[3])
+            if k >= OUT_DELAY:
+                output(*steps[k - OUT_DELAY])

@@ -19,7 +19,7 @@ PAIRS = 4
 BLOCKS = 16
 FLOPS = 2 * 2 * 384 * 4096 * 1536
 RAW_BUFS = 8
-OUT_DELAY = 2
+OUTPUTS_AFTER = {3: (0, 1), 5: (2, 3), 6: (4, 5), 7: (6, 7)}
 GATE_ORDER = (1, 0, 2, 3)
 GATE_FUNC = (ACT.Sigmoid, ACT.Sigmoid, ACT.Tanh, ACT.Sigmoid)
 
@@ -239,7 +239,7 @@ def tile_odelstmcell_pa_kernel(tc, inputs, h0, c0, w_ih, w_hh, b_ih, b_hh, out_0
             return slice(0, NA) if part == 0 else slice(NA, NB)
 
         def pair_act(b, gi, part, banks):
-            a = gact.tile([P, 2, (NA, P)[part]], F32, tag="g%d" % gi)
+            a = gact.tile([P, 2, (NA, P)[part]], F32, tag="g%d" % gi, bufs=(3, 3, 3, 4)[gi])
             for e in range(2):
                 act(a[:, e, :], banks[e], gi, 2 * b + e)
             pa[(b, gi, part)] = a
@@ -282,52 +282,61 @@ def tile_odelstmcell_pa_kernel(tc, inputs, h0, c0, w_ih, w_hh, b_ih, b_hh, out_0
                 (g + 1) * n,
             )
 
-        tb = transposes(0)
-        grp = grpp.tile([P, 6 * 2 * P], F32, tag="grp", align_bytes=64)
-        for k in range(3):
-            evac_bank("SVS"[k], grp, k, tb[k])
-        quantise_block(0, grp)
-        bias_prep()
-        for q in range(BLOCKS):
+        runs = [((0, 1), (0,)), ((2, 3), (1,))]
+        runs += [((n, n + 1), (n - 2, n - 1)) for n in range(4, BLOCKS, 2)]
+        runs.append(((), (BLOCKS - 2, BLOCKS - 1)))
+
+        def step_of(q):
             b, o = divmod(q, 4)
-            gi = GATE_ORDER[o]
-            more = q + 1 < BLOCKS
-            if more:
-                tb = transposes(q + 1)
-            if o == 1:
-                c0_prep_a(b)
-            if more:
-                if q + RAW_BUFS < BLOCKS:
-                    load_block(q + RAW_BUFS)
-                grp = grpp.tile([P, 6 * 2 * P], F32, tag="grp", align_bytes=64)
-                evac_bank("S", grp, 0, tb[0])
-                evac_bank("V", grp, 1, tb[1])
             if o == 0 and b > 0:
-                pair_add(b - 1, 0)
+                return lambda: pair_ig(b - 1, 0)
             if o == 1 and b > 0:
-                pair_h(b - 1, 0)
+                return lambda: pair_add(b - 1, 0)
             if o == 2:
-                pair_fc(b, 0, 0)
-            if o == 3:
-                pair_ig(b, 0)
-            if more:
-                evac_bank("S", grp, 2, tb[2])
-            if o == 0 and b > 0:
-                pair_tanh(b - 1, 0)
-            if more:
-                quantise_block(q + 1, grp)
-            if q == 10:
+                return lambda: pair_fc(b, 0, 0)
+            if o == 3 and b > 0:
+                return lambda: pair_h(b - 1, 0)
+            return lambda: None
+
+        for new, old in runs:
+            banks = {}
+            for n in new:
+                banks[n] = transposes(n)
+            for q in old:
+                if q % 4 == 1:
+                    c0_prep_a(q // 4)
+            for q in old:
+                if q % 4 == 2 and q > 4:
+                    pair_tanh(q // 4 - 1, 0)
+            for n in new:
+                if n + RAW_BUFS < BLOCKS:
+                    load_block(n + RAW_BUFS)
+            ops = [step_of(q) for q in old]
+            for i, n in enumerate(new):
+                grp = grpp.tile([P, 6 * 2 * P], F32, tag="grp", align_bytes=64)
+                for k in range(3):
+                    evac_bank("SVS"[k], grp, k, banks[n][k])
+                if i < len(ops):
+                    ops[i]()
+                quantise_block(n, grp)
+            for i in range(len(new), len(ops)):
+                ops[i]()
+            if 0 in old:
+                bias_prep()
+            if 12 in old:
                 h1_quant(0, 0)
-            gt = psum.tile([P, 2, NA], F32, tag="bank")
-            for e in range(2):
-                passes(gt[:, e, :], 2 * b + e, gi, 0, 0)
-            pair_act(b, gi, 0, [gt[:, e, :] for e in range(2)])
-            if q == 11:
+            for q in old:
+                b, o = divmod(q, 4)
+                gt = psum.tile([P, 2, NA], F32, tag="bank")
+                for e in range(2):
+                    passes(gt[:, e, :], 2 * b + e, GATE_ORDER[o], 0, 0)
+                pair_act(b, GATE_ORDER[o], 0, [gt[:, e, :] for e in range(2)])
+            if 9 in old:
                 acts_b_prep()
-            if q == 12:
+            if 11 in old:
                 c0_prep_b()
+        pair_ig(PAIRS - 1, 0)
         pair_add(PAIRS - 1, 0)
-        pair_tanh(PAIRS - 1, 0)
 
         def gate_mx(b, part, cell):
             n = (NA, P)[part]
@@ -344,26 +353,29 @@ def tile_odelstmcell_pa_kernel(tc, inputs, h0, c0, w_ih, w_hh, b_ih, b_hh, out_0
 
         for b in range(PAIRS):
             gt = gate_mx(b, 1, 0)
-            if b == 0:
-                pair_h(PAIRS - 1, 0)
-                h1_quant(1, 0)
             pair_act(b, 1, 1, gt[1])
             pair_act(b, 0, 1, gt[0])
+            if b == 0:
+                pair_tanh(PAIRS - 1, 0)
             pair_fc(b, 1, 0)
+            if b == 0:
+                pair_h(PAIRS - 1, 0)
+            pair_act(b, 2, 1, gt[2])
+            pair_act(b, 3, 1, gt[3])
+            pair_ig(b, 1)
+            pair_add(b, 1)
+            if b == 0:
+                h1_quant(1, 0)
             if b > 0:
                 pair_tanh(b - 1, 1)
                 pair_h(b - 1, 1)
-                if b == 2:
-                    h1_quant(0, 1)
-            pair_act(b, 2, 1, gt[2])
-            pair_ig(b, 1)
-            pair_add(b, 1)
-            pair_act(b, 3, 1, gt[3])
+            if b == 2:
+                h1_quant(0, 1)
         pair_tanh(PAIRS - 1, 1)
         pair_h(PAIRS - 1, 1)
         h1_quant(1, 1)
 
-        def output(b, part):
+        def output_transposes(b, part):
             nt = 2 - part
             c_ps = psum.tile([P, nt, 2, P], F32, tag="bank")
             o_ps = psum.tile([P, nt, 2, P], F32, tag="bank")
@@ -374,6 +386,10 @@ def tile_odelstmcell_pa_kernel(tc, inputs, h0, c0, w_ih, w_hh, b_ih, b_hh, out_0
             for t in range(nt):
                 for e in range(2):
                     nc.tensor.transpose(o_ps[:, t, e, :], pa[(b, 3, part)][:, e, 128 * t : 128 * t + 128], ident[:])
+            return c_ps, o_ps
+
+        def output_store(b, part, c_ps, o_ps):
+            nt = 2 - part
             c_sb = outp.tile([P, nt, 2 * P], F32, tag="c%d" % part)
             h_sb = outp.tile([P, nt, 2 * P], F32, tag="h%d" % part)
             th = outp.tile([P, nt, 2, P], F32, tag="t%d" % part)
@@ -393,16 +409,16 @@ def tile_odelstmcell_pa_kernel(tc, inputs, h0, c0, w_ih, w_hh, b_ih, b_hh, out_0
                     nc.sync.dma_start(out=rows_b(dram)[:, 256 * b : 256 * b + 256], in_=sb[:, 0, :])
 
         steps = [(b, part) for b0 in (0, 2) for part in range(2) for b in (b0, b0 + 1)]
-        for k in range(len(steps) + OUT_DELAY):
-            if k < len(steps):
-                b, part = steps[k]
-                gt = gate_mx(b, part, 1)
-                pair_act(b, 1, part, gt[1])
-                pair_fc(b, part, 1)
-                pair_act(b, 0, part, gt[0])
-                pair_act(b, 2, part, gt[2])
-                pair_ig(b, part)
-                pair_add(b, part)
-                pair_act(b, 3, part, gt[3])
-            if k >= OUT_DELAY:
-                output(*steps[k - OUT_DELAY])
+        for k, (b, part) in enumerate(steps):
+            gt = gate_mx(b, part, 1)
+            pair_act(b, 1, part, gt[1])
+            pair_fc(b, part, 1)
+            pair_act(b, 0, part, gt[0])
+            pair_act(b, 2, part, gt[2])
+            pair_ig(b, part)
+            pair_add(b, part)
+            pair_act(b, 3, part, gt[3])
+            done = [steps[i] for i in OUTPUTS_AFTER.get(k, ())]
+            banks = [output_transposes(*step) for step in done]
+            for step, (c_ps, o_ps) in zip(done, banks):
+                output_store(*step, c_ps, o_ps)

@@ -41,13 +41,15 @@ def tile_odelstmcell_pa_kernel(tc, inputs, h0, c0, w_ih, w_hh, b_ih, b_hh, out_0
             else:
                 nc.vector.tensor_copy(out=out, in_=in_)
 
+        bias_raw = const.tile([P, 256], BF16)
+        nc.vector.memset(bias_raw[:], 0.0)
+        nc.scalar.dma_start(out=bias_raw[0:16, :], in_=b_ih.rearrange("(r c) -> r c", c=256))
+        nc.scalar.dma_start(out=bias_raw[16:32, :], in_=b_hh.rearrange("(r c) -> r c", c=256))
         warm = const.tile([P, 1], F32)
         nc.vector.memset(warm[:], 0.0)
         nc.scalar.activation(out=warm[:], in_=warm[:], func=ACT.Sigmoid)
         ident = const.tile([P, P], F32)
         make_identity(nc, ident[:])
-        bias_raw = const.tile([P, 256], BF16)
-        nc.vector.memset(bias_raw[:], 0.0)
 
         def rows_a(x):
             return x[0:NA, :].rearrange("(p t) k -> p t k", t=2)
@@ -79,11 +81,9 @@ def tile_odelstmcell_pa_kernel(tc, inputs, h0, c0, w_ih, w_hh, b_ih, b_hh, out_0
 
         nc.sync.dma_start(out=xa_raw[:], in_=rows_a(inputs))
         nc.sync.dma_start(out=ha_raw[:], in_=rows_a(h0))
-        nc.scalar.dma_start(out=bias_raw[0:16, :], in_=b_ih.rearrange("(r c) -> r c", c=256))
-        nc.scalar.dma_start(out=bias_raw[16:32, :], in_=b_hh.rearrange("(r c) -> r c", c=256))
         for q in range(RAW_BUFS):
             load_block(q)
-            if q == 1:
+            if q == 3:
                 nc.sync.dma_start(out=ca_raw[:], in_=rows_a(c0))
         nc.sync.dma_start(out=xb_raw[:], in_=rows_b(inputs))
         nc.sync.dma_start(out=hb_raw[:], in_=rows_b(h0))
@@ -142,6 +142,8 @@ def tile_odelstmcell_pa_kernel(tc, inputs, h0, c0, w_ih, w_hh, b_ih, b_hh, out_0
             nc.vector.tensor_copy(out=bias_w[:], in_=tp[:, 0, 0, 0:32])
             bias_wb = bias_w[:].bitcast(BF16)
             nc.vector.tensor_tensor(out=bias[:], in0=bias_wb[:, 0:32], in1=bias_wb[:, 32:64], op=ALU.add)
+
+        bias_prep()
 
         def acts_b_prep():
             aB_grp4 = aB_grp[:].rearrange("p (s m u) -> p s m u", s=3, u=2)
@@ -315,14 +317,12 @@ def tile_odelstmcell_pa_kernel(tc, inputs, h0, c0, w_ih, w_hh, b_ih, b_hh, out_0
             for i, n in enumerate(new):
                 grp = grpp.tile([P, 6 * 2 * P], F32, tag="grp", align_bytes=64)
                 for k in range(3):
-                    evac_bank("SVS"[k], grp, k, banks[n][k])
+                    evac_bank("V" if k == 1 and n % 2 == 0 else "S", grp, k, banks[n][k])
                 if i < len(ops):
                     ops[i]()
                 quantise_block(n, grp)
             for i in range(len(new), len(ops)):
                 ops[i]()
-            if 0 in old:
-                bias_prep()
             if 12 in old:
                 h1_quant(0, 0)
             for q in old:

@@ -73,7 +73,12 @@ def tile_odelstmcell_pa_kernel(tc, inputs, h0, c0, w_ih, w_hh, b_ih, b_hh, out_0
             wih_raw = rawp.tile([P, 2 * 512], BF16, tag="wih")
             nc.sync.dma_start(out=wih_raw[:], in_=wih_v[b, gi])
             whh_raw = rawp.tile([P, 2 * 1024], BF16, tag="whh")
-            nc.sync.dma_start(out=whh_raw[:], in_=whh_v[b, gi])
+            parts = 2 if q < 2 else 1
+            width = 2 * 1024 // parts
+            for i in range(parts):
+                nc.sync.dma_start(
+                    out=whh_raw[:, i * width : (i + 1) * width], in_=whh_v[b, gi][:, i * width : (i + 1) * width]
+                )
             raw_views[q] = (
                 wih_raw[:].bitcast(F32).rearrange("p (e w) -> p e w", e=2),
                 whh_raw[:].bitcast(F32).rearrange("p (e w) -> p e w", e=2),
@@ -83,7 +88,7 @@ def tile_odelstmcell_pa_kernel(tc, inputs, h0, c0, w_ih, w_hh, b_ih, b_hh, out_0
         nc.sync.dma_start(out=ha_raw[:], in_=rows_a(h0))
         for q in range(RAW_BUFS):
             load_block(q)
-            if q == 3:
+            if q == 2:
                 nc.sync.dma_start(out=ca_raw[:], in_=rows_a(c0))
         nc.sync.dma_start(out=xb_raw[:], in_=rows_b(inputs))
         nc.sync.dma_start(out=hb_raw[:], in_=rows_b(h0))
@@ -284,8 +289,8 @@ def tile_odelstmcell_pa_kernel(tc, inputs, h0, c0, w_ih, w_hh, b_ih, b_hh, out_0
                 (g + 1) * n,
             )
 
-        runs = [((0, 1), (0,)), ((2, 3), (1,))]
-        runs += [((n, n + 1), (n - 2, n - 1)) for n in range(4, BLOCKS, 2)]
+        runs = [((0, 1), (0,)), ((2,), (1,)), ((3,), (2,)), ((4, 5), (3,))]
+        runs += [((n, n + 1), (n - 2, n - 1)) for n in range(6, BLOCKS, 2)]
         runs.append(((), (BLOCKS - 2, BLOCKS - 1)))
 
         def step_of(q):

@@ -19,7 +19,7 @@ PAIRS = 4
 BLOCKS = 16
 FLOPS = 2 * 2 * 384 * 4096 * 1536
 RAW_BUFS = 8
-OUTPUTS_AFTER = {3: (0, 1), 5: (2, 3), 6: (4, 5), 7: (6, 7)}
+OUTPUTS_AFTER = {3: (0, 1), 5: (2, 3, 4), 6: (5,), 7: (6, 7)}
 GATE_ORDER = (1, 0, 2, 3)
 GATE_FUNC = (ACT.Sigmoid, ACT.Sigmoid, ACT.Tanh, ACT.Sigmoid)
 
@@ -386,22 +386,20 @@ def tile_odelstmcell_pa_kernel(tc, inputs, h0, c0, w_ih, w_hh, b_ih, b_hh, out_0
             o_ps = psum.tile([P, nt, 2, P], F32, tag="bank")
             for t in range(nt):
                 for e in range(2):
-                    lo = NA * part + 128 * t
-                    nc.tensor.transpose(c_ps[:, t, e, :], c_st[:, 2 * b + e, lo : lo + 128], ident[:])
+                    nc.tensor.transpose(o_ps[:, t, e, :], pa[(b, 3, part)][:, e, 128 * t : 128 * t + 128], ident[:])
             for t in range(nt):
                 for e in range(2):
-                    nc.tensor.transpose(o_ps[:, t, e, :], pa[(b, 3, part)][:, e, 128 * t : 128 * t + 128], ident[:])
+                    lo = NA * part + 128 * t
+                    nc.tensor.transpose(c_ps[:, t, e, :], c_st[:, 2 * b + e, lo : lo + 128], ident[:])
             return c_ps, o_ps
 
-        def output_store(b, part, c_ps, o_ps):
+        def output_store(b, part, c_ps, o_ps, who):
             nt = 2 - part
             c_sb = outp.tile([P, nt, 2 * P], F32, tag="c%d" % part)
             h_sb = outp.tile([P, nt, 2 * P], F32, tag="h%d" % part)
             th = outp.tile([P, nt, 2, P], F32, tag="t%d" % part)
             nc.scalar.activation(out=th[:], in_=c_ps[:], func=ACT.Tanh)
-            nc.vector.tensor_copy(
-                out=c_sb[:].rearrange("p t (m e) -> p t m e", e=2), in_=c_ps[:].rearrange("p t e m -> p t m e")
-            )
+            evac(who, c_sb[:].rearrange("p t (m e) -> p t m e", e=2), c_ps[:].rearrange("p t e m -> p t m e"))
             mult(
                 h_sb[:].rearrange("p t (m e) -> p t m e", e=2),
                 o_ps[:].rearrange("p t e m -> p t m e"),
@@ -426,4 +424,4 @@ def tile_odelstmcell_pa_kernel(tc, inputs, h0, c0, w_ih, w_hh, b_ih, b_hh, out_0
             done = [steps[i] for i in OUTPUTS_AFTER.get(k, ())]
             banks = [output_transposes(*step) for step in done]
             for step, (c_ps, o_ps) in zip(done, banks):
-                output_store(*step, c_ps, o_ps)
+                output_store(*step, c_ps, o_ps, "S" if k == len(steps) - 1 else "V")

@@ -67,6 +67,11 @@ def tile_odelstmcell_pa_kernel(tc, inputs, h0, c0, w_ih, w_hh, b_ih, b_hh, out_0
         whh_v = w_hh.rearrange("(g b p e) k -> b g p (e k)", g=4, b=4, p=P, e=2)
         raw_views = {}
 
+        def load_b():
+            nc.sync.dma_start(out=xb_raw[:], in_=rows_b(inputs))
+            nc.sync.dma_start(out=hb_raw[:], in_=rows_b(h0))
+            nc.sync.dma_start(out=cb_raw[:], in_=rows_b(c0))
+
         def load_block(q):
             b, o = divmod(q, 4)
             gi = GATE_ORDER[o]
@@ -88,11 +93,10 @@ def tile_odelstmcell_pa_kernel(tc, inputs, h0, c0, w_ih, w_hh, b_ih, b_hh, out_0
         nc.sync.dma_start(out=ha_raw[:], in_=rows_a(h0))
         for q in range(RAW_BUFS):
             load_block(q)
-            if q == 2:
+            if q == 7:
                 nc.sync.dma_start(out=ca_raw[:], in_=rows_a(c0))
-        nc.sync.dma_start(out=xb_raw[:], in_=rows_b(inputs))
-        nc.sync.dma_start(out=hb_raw[:], in_=rows_b(h0))
-        nc.sync.dma_start(out=cb_raw[:], in_=rows_b(c0))
+            if q == 11:
+                load_b()
         xa_f = xa_raw[:].rearrange("p t k -> p (t k)").bitcast(F32).rearrange("p (t w) -> p t w", t=2)
         ha_f = ha_raw[:].rearrange("p t k -> p (t k)").bitcast(F32).rearrange("p (t w) -> p t w", t=2)
         ca_f = ca_raw[:].rearrange("p t k -> p (t k)").bitcast(F32).rearrange("p (t w) -> p t w", t=2)
@@ -298,8 +302,10 @@ def tile_odelstmcell_pa_kernel(tc, inputs, h0, c0, w_ih, w_hh, b_ih, b_hh, out_0
             if o == 0 and b > 0:
                 return lambda: pair_ig(b - 1, 0)
             if o == 1 and b > 0:
+                if b == 1:
+                    return lambda: (pair_fc(0, 0, 0), pair_add(0, 0))
                 return lambda: pair_add(b - 1, 0)
-            if o == 2:
+            if o == 2 and b > 0:
                 return lambda: pair_fc(b, 0, 0)
             if o == 3 and b > 0:
                 return lambda: pair_h(b - 1, 0)
@@ -310,14 +316,16 @@ def tile_odelstmcell_pa_kernel(tc, inputs, h0, c0, w_ih, w_hh, b_ih, b_hh, out_0
             for n in new:
                 banks[n] = transposes(n)
             for q in old:
-                if q % 4 == 1:
-                    c0_prep_a(q // 4)
+                if q % 4 == 1 and q > 1 or q == 4:
+                    c0_prep_a(0 if q == 4 else q // 4)
             for q in old:
                 if q % 4 == 2 and q > 4:
                     pair_tanh(q // 4 - 1, 0)
             for n in new:
                 if n + RAW_BUFS < BLOCKS:
                     load_block(n + RAW_BUFS)
+                if n + RAW_BUFS == 11:
+                    load_b()
             ops = [step_of(q) for q in old]
             for i, n in enumerate(new):
                 grp = grpp.tile([P, 6 * 2 * P], F32, tag="grp", align_bytes=64)

@@ -19,7 +19,7 @@ PAIRS = 4
 BLOCKS = 16
 FLOPS = 2 * 2 * 384 * 4096 * 1536
 RAW_BUFS = 8
-OUTPUTS_AFTER = {3: (0, 1), 5: (2, 3, 4), 6: (5,), 7: (6, 7)}
+OUTPUTS_AFTER = {3: (0, 1), 5: (2, 3, 4)}
 GATE_ORDER = (1, 0, 2, 3)
 GATE_FUNC = (ACT.Sigmoid, ACT.Sigmoid, ACT.Tanh, ACT.Sigmoid)
 
@@ -420,7 +420,7 @@ def tile_odelstmcell_pa_kernel(tc, inputs, h0, c0, w_ih, w_hh, b_ih, b_hh, out_0
                     nc.sync.dma_start(out=rows_b(dram)[:, 256 * b : 256 * b + 256], in_=sb[:, 0, :])
 
         steps = [(b, part) for b0 in (0, 2) for part in range(2) for b in (b0, b0 + 1)]
-        for k, (b, part) in enumerate(steps):
+        for k, (b, part) in enumerate(steps[:-2]):
             gt = gate_mx(b, part, 1)
             pair_act(b, 1, part, gt[1])
             pair_fc(b, part, 1)
@@ -432,4 +432,55 @@ def tile_odelstmcell_pa_kernel(tc, inputs, h0, c0, w_ih, w_hh, b_ih, b_hh, out_0
             done = [steps[i] for i in OUTPUTS_AFTER.get(k, ())]
             banks = [output_transposes(*step) for step in done]
             for step, (c_ps, o_ps) in zip(done, banks):
-                output_store(*step, c_ps, o_ps, "S" if k == len(steps) - 1 else "V")
+                output_store(*step, c_ps, o_ps, "V")
+
+        def gate_bank(*which):
+            bank = psum.tile([P, 4, P], F32, tag="bank")
+            for l, (b, gi) in enumerate(which):
+                for e in range(2):
+                    passes(bank[:, 2 * l + e, :], 2 * b + e, gi, 1, 1)
+            return [[bank[:, 2 * l + e, :] for e in range(2)] for l in range(2)]
+
+        b0, b1 = PAIRS - 2, PAIRS - 1
+        f0, i0 = gate_bank((b0, 1), (b0, 0))
+        g0, g1 = gate_bank((b0, 2), (b1, 2))
+        f1, i1 = gate_bank((b1, 1), (b1, 0))
+        pair_act(b0, 1, 1, f0)
+        pair_fc(b0, 1, 1)
+        pair_act(b0, 0, 1, i0)
+        pair_act(b0, 2, 1, g0)
+        pair_ig(b0, 1)
+        pair_add(b0, 1)
+        pair_act(b1, 2, 1, g1)
+        pair_act(b1, 1, 1, f1)
+        pair_fc(b1, 1, 1)
+        pair_act(b1, 0, 1, i1)
+        pair_ig(b1, 1)
+        pair_add(b1, 1)
+        c_ps, o_ps = output_transposes(b1, 0)
+        output_store(b1, 0, c_ps, o_ps, "V")
+        o0, o1 = gate_bank((b0, 3), (b1, 3))
+        pair_act(b0, 3, 1, o0)
+        pair_act(b1, 3, 1, o1)
+        c_ps = psum.tile([P, 2, 2, P], F32, tag="bank")
+        o_ps = psum.tile([P, 2, 2, P], F32, tag="bank")
+        for i, b in enumerate((b0, b1)):
+            for e in range(2):
+                nc.tensor.transpose(c_ps[:, i, e, :], c_st[:, 2 * b + e, NA:NB], ident[:])
+        for i, b in enumerate((b0, b1)):
+            for e in range(2):
+                nc.tensor.transpose(o_ps[:, i, e, :], pa[(b, 3, 1)][:, e, :], ident[:])
+        c_sb = outp.tile([P, 4 * P], F32, tag="c0")
+        h_sb = outp.tile([P, 4 * P], F32, tag="h0")
+        th = outp.tile([P, 2, 2, P], F32, tag="t0")
+        for i in range(2):
+            nc.scalar.activation(out=th[:, i], in_=c_ps[:, i], func=ACT.Tanh)
+        evac("V", c_sb[:].rearrange("p (i m e) -> p i m e", i=2, e=2), c_ps[:].rearrange("p i e m -> p i m e"))
+        nc.sync.dma_start(out=rows_b(out_1)[:, 512:1024], in_=c_sb[:])
+        for i in range(2):
+            mult(
+                h_sb[:, 256 * i : 256 * i + 256].rearrange("p (m e) -> p m e", e=2),
+                o_ps[:, i].rearrange("p e m -> p m e"),
+                th[:, i].rearrange("p e m -> p m e"),
+            )
+        nc.sync.dma_start(out=rows_b(out_0)[:, 512:1024], in_=h_sb[:])

@@ -19,7 +19,8 @@ PAIRS = 4
 BLOCKS = 16
 FLOPS = 2 * 2 * 384 * 4096 * 1536
 RAW_BUFS = 8
-OUTPUTS_AFTER = {3: (0, 1), 5: (2, 3, 4)}
+OUTPUTS_AFTER = {3: (1,), 5: (2, 3, 4)}
+VECTOR_AFTER = {1: (0,)}
 GATE_ORDER = (1, 0, 2, 3)
 GATE_FUNC = (ACT.Sigmoid, ACT.Sigmoid, ACT.Tanh, ACT.Sigmoid)
 
@@ -75,7 +76,7 @@ def tile_odelstmcell_pa_kernel(tc, inputs, h0, c0, w_ih, w_hh, b_ih, b_hh, out_0
         def load_block(q):
             b, o = divmod(q, 4)
             gi = GATE_ORDER[o]
-            wih_raw = rawp.tile([P, 2 * 512], BF16, tag="wih")
+            wih_raw = rawp.tile([P, 2 * 512], BF16, tag="wih", align_bytes=64)
             nc.sync.dma_start(out=wih_raw[:], in_=wih_v[b, gi])
             whh_raw = rawp.tile([P, 2 * 1024], BF16, tag="whh")
             parts = 2 if q < 2 else 1
@@ -119,7 +120,9 @@ def tile_odelstmcell_pa_kernel(tc, inputs, h0, c0, w_ih, w_hh, b_ih, b_hh, out_0
         hB_scales = const.tile([P, 2 * P], U8, align_bytes=64)
         c0B = const.tile([P, PAIRS * P], F32)
         c0B_bf = c0B[:].bitcast(BF16).rearrange("p (b n e) -> p b e n", b=PAIRS, e=2)
-        c_st = const.tile([P, UNITS, NB], F32)
+        cA_st = const.tile([P, UNITS, NA], F32, align_bytes=64)
+        cB_st = const.tile([P, UNITS, P], F32, align_bytes=64)
+        c_st = (cA_st, cB_st)
         w_codes = const.tile([P, 96 * P], U32, align_bytes=64)
         w_scales = const.tile([P, 96 * P], U8, align_bytes=64)
         bias_w = const.tile([P, 32], F32)
@@ -258,7 +261,7 @@ def tile_odelstmcell_pa_kernel(tc, inputs, h0, c0, w_ih, w_hh, b_ih, b_hh, out_0
         def pair_fc(b, part, cell):
             a = pa[(b, 1, part)]
             if cell == 1:
-                c = c_st[:, 2 * b : 2 * b + 2, cols(part)]
+                c = c_st[part][:, 2 * b : 2 * b + 2, :]
             else:
                 c = c0_psum[b] if part == 0 else c0B_bf[:, b]
             mult(a[:], a[:], c)
@@ -269,12 +272,20 @@ def tile_odelstmcell_pa_kernel(tc, inputs, h0, c0, w_ih, w_hh, b_ih, b_hh, out_0
 
         def pair_add(b, part):
             nc.vector.tensor_tensor(
-                out=c_st[:, 2 * b : 2 * b + 2, cols(part)], in0=pa[(b, 1, part)][:], in1=pa[(b, 0, part)][:], op=ALU.add
+                out=c_st[part][:, 2 * b : 2 * b + 2, :], in0=pa[(b, 1, part)][:], in1=pa[(b, 0, part)][:], op=ALU.add
             )
+
+        def pair_ig_add(b, part):
+            f, i, g = (pa[(b, x, part)] for x in (1, 0, 2))
+            for e in range(2):
+                mult(i[:, e, :], i[:, e, :], g[:, e, :])
+            for e in range(2):
+                c = c_st[part][:, 2 * b + e, :]
+                nc.vector.tensor_tensor(out=c, in0=f[:, e, :], in1=i[:, e, :], op=ALU.add)
 
         def pair_tanh(b, part):
             nc.scalar.activation(
-                out=pa[(b, 2, part)][:], in_=c_st[:, 2 * b : 2 * b + 2, cols(part)], func=ACT.Tanh
+                out=pa[(b, 2, part)][:], in_=c_st[part][:, 2 * b : 2 * b + 2, :], func=ACT.Tanh
             )
 
         def pair_h(b, part):
@@ -375,8 +386,7 @@ def tile_odelstmcell_pa_kernel(tc, inputs, h0, c0, w_ih, w_hh, b_ih, b_hh, out_0
                 pair_h(PAIRS - 1, 0)
             pair_act(b, 2, 1, gt[2])
             pair_act(b, 3, 1, gt[3])
-            pair_ig(b, 1)
-            pair_add(b, 1)
+            pair_ig_add(b, 1)
             if b == 0:
                 h1_quant(1, 0)
             if b > 0:
@@ -397,8 +407,7 @@ def tile_odelstmcell_pa_kernel(tc, inputs, h0, c0, w_ih, w_hh, b_ih, b_hh, out_0
                     nc.tensor.transpose(o_ps[:, t, e, :], pa[(b, 3, part)][:, e, 128 * t : 128 * t + 128], ident[:])
             for t in range(nt):
                 for e in range(2):
-                    lo = NA * part + 128 * t
-                    nc.tensor.transpose(c_ps[:, t, e, :], c_st[:, 2 * b + e, lo : lo + 128], ident[:])
+                    nc.tensor.transpose(c_ps[:, t, e, :], c_st[part][:, 2 * b + e, 128 * t : 128 * t + 128], ident[:])
             return c_ps, o_ps
 
         def output_store(b, part, c_ps, o_ps, who):
@@ -419,6 +428,31 @@ def tile_odelstmcell_pa_kernel(tc, inputs, h0, c0, w_ih, w_hh, b_ih, b_hh, out_0
                 else:
                     nc.sync.dma_start(out=rows_b(dram)[:, 256 * b : 256 * b + 256], in_=sb[:, 0, :])
 
+        def vector_store(b, part):
+            n = (NA, P)[part]
+            pair_tanh(b, part)
+            turned = {}
+            h = rawp.tile([P, 2 * n], F32, tag="wih", align_bytes=64)
+            ct = rawp.tile([P, 2 * n], F32, tag="wih", align_bytes=64)
+            ht = rawp.tile([P, 2 * n], F32, tag="wih", align_bytes=64)
+            c_sb = outp.tile([P, 2 * n], F32, tag="c%d" % part)
+            h_sb = outp.tile([P, 2 * n], F32, tag="h%d" % part)
+            nc.vector.transpose(ct[:], c_st[part][:, 2 * b : 2 * b + 2, :].rearrange("p e n -> p (e n)"))
+            mult(h[:], pa[(b, 3, part)][:].rearrange("p e n -> p (e n)"), pa[(b, 2, part)][:].rearrange("p e n -> p (e n)"))
+            nc.vector.tensor_copy(out=c_sb[:].rearrange("p (m e) -> p m e", e=2), in_=ct[:].rearrange("p (e m) -> p m e", e=2))
+            nc.vector.transpose(ht[:], h[:])
+            for dram, sb, src in ((out_1, c_sb, None), (out_0, h_sb, ht)):
+                if src is not None:
+                    nc.vector.tensor_copy(out=sb[:].rearrange("p (m e) -> p m e", e=2), in_=src[:].rearrange("p (e m) -> p m e", e=2))
+                rows = dram[0:NA, :].rearrange("(c r t) k -> t r c k", r=32, t=2)
+                for q in range(4):
+                    lo = 256 * b + 64 * q
+                    for t in range(2):
+                        nc.sync.dma_start(
+                            out=rows[t][:, :, lo : lo + 64],
+                            in_=sb[32 * q : 32 * q + 32, 256 * t : 256 * t + 256].rearrange("p (c k) -> p c k", k=64),
+                        )
+
         steps = [(b, part) for b0 in (0, 2) for part in range(2) for b in (b0, b0 + 1)]
         for k, (b, part) in enumerate(steps[:-2]):
             gt = gate_mx(b, part, 1)
@@ -426,9 +460,10 @@ def tile_odelstmcell_pa_kernel(tc, inputs, h0, c0, w_ih, w_hh, b_ih, b_hh, out_0
             pair_fc(b, part, 1)
             pair_act(b, 0, part, gt[0])
             pair_act(b, 2, part, gt[2])
-            pair_ig(b, part)
-            pair_add(b, part)
+            pair_ig_add(b, part)
             pair_act(b, 3, part, gt[3])
+            for i in VECTOR_AFTER.get(k, ()):
+                vector_store(*steps[i])
             done = [steps[i] for i in OUTPUTS_AFTER.get(k, ())]
             banks = [output_transposes(*step) for step in done]
             for step, (c_ps, o_ps) in zip(done, banks):
@@ -449,14 +484,12 @@ def tile_odelstmcell_pa_kernel(tc, inputs, h0, c0, w_ih, w_hh, b_ih, b_hh, out_0
         pair_fc(b0, 1, 1)
         pair_act(b0, 0, 1, i0)
         pair_act(b0, 2, 1, g0)
-        pair_ig(b0, 1)
-        pair_add(b0, 1)
+        pair_ig_add(b0, 1)
         pair_act(b1, 2, 1, g1)
         pair_act(b1, 1, 1, f1)
         pair_fc(b1, 1, 1)
         pair_act(b1, 0, 1, i1)
-        pair_ig(b1, 1)
-        pair_add(b1, 1)
+        pair_ig_add(b1, 1)
         c_ps, o_ps = output_transposes(b1, 0)
         output_store(b1, 0, c_ps, o_ps, "V")
         o0, o1 = gate_bank((b0, 3), (b1, 3))
@@ -466,7 +499,7 @@ def tile_odelstmcell_pa_kernel(tc, inputs, h0, c0, w_ih, w_hh, b_ih, b_hh, out_0
         o_ps = psum.tile([P, 2, 2, P], F32, tag="bank")
         for i, b in enumerate((b0, b1)):
             for e in range(2):
-                nc.tensor.transpose(c_ps[:, i, e, :], c_st[:, 2 * b + e, NA:NB], ident[:])
+                nc.tensor.transpose(c_ps[:, i, e, :], c_st[1][:, 2 * b + e, :], ident[:])
         for i, b in enumerate((b0, b1)):
             for e in range(2):
                 nc.tensor.transpose(o_ps[:, i, e, :], pa[(b, 3, 1)][:, e, :], ident[:])

@@ -60,7 +60,8 @@ def tile_odelstmcell_pa_kernel(tc, inputs, h0, c0, w_ih, w_hh, b_ih, b_hh, out_0
 
         xa_raw = const.tile([P, 2, 512], BF16)
         ha_raw = const.tile([P, 2, 1024], BF16)
-        ca_raw = const.tile([P, 2, 1024], BF16)
+        ca0_raw = const.tile([P, 2, 512], BF16)
+        ca1_raw = const.tile([P, 2, 512], BF16)
         xb_raw = const.tile([P, 512], BF16)
         hb_raw = const.tile([P, 1024], BF16)
         cb_raw = const.tile([P, 1024], BF16)
@@ -72,6 +73,10 @@ def tile_odelstmcell_pa_kernel(tc, inputs, h0, c0, w_ih, w_hh, b_ih, b_hh, out_0
             nc.sync.dma_start(out=xb_raw[:], in_=rows_b(inputs))
             nc.sync.dma_start(out=hb_raw[:], in_=rows_b(h0))
             nc.sync.dma_start(out=cb_raw[:], in_=rows_b(c0))
+
+        def load_ca(half):
+            lo = 512 * half
+            nc.sync.dma_start(out=(ca0_raw, ca1_raw)[half][:], in_=rows_a(c0)[:, :, lo : lo + 512])
 
         def load_block(q):
             b, o = divmod(q, 4)
@@ -95,12 +100,14 @@ def tile_odelstmcell_pa_kernel(tc, inputs, h0, c0, w_ih, w_hh, b_ih, b_hh, out_0
         for q in range(RAW_BUFS):
             load_block(q)
             if q == 7:
-                nc.sync.dma_start(out=ca_raw[:], in_=rows_a(c0))
-            if q == 11:
+                load_ca(0)
+            if q == 13:
                 load_b()
         xa_f = xa_raw[:].rearrange("p t k -> p (t k)").bitcast(F32).rearrange("p (t w) -> p t w", t=2)
         ha_f = ha_raw[:].rearrange("p t k -> p (t k)").bitcast(F32).rearrange("p (t w) -> p t w", t=2)
-        ca_f = ca_raw[:].rearrange("p t k -> p (t k)").bitcast(F32).rearrange("p (t w) -> p t w", t=2)
+        ca_f = [
+            raw[:].rearrange("p t k -> p (t k)").bitcast(F32).rearrange("p (t w) -> p t w", t=2) for raw in (ca0_raw, ca1_raw)
+        ]
         xb_f = xb_raw[:].bitcast(F32)
         hb_f = hb_raw[:].bitcast(F32)
         cb_f = cb_raw[:].bitcast(F32)
@@ -176,7 +183,7 @@ def tile_odelstmcell_pa_kernel(tc, inputs, h0, c0, w_ih, w_hh, b_ih, b_hh, out_0
         def c0_prep_a(b):
             tp = psum.tile([P, NA], F32, tag="bank")
             for t in range(2):
-                nc.tensor.transpose(tp[:, 128 * t : 128 * t + 128], ca_f[:, t, 128 * b : 128 * b + 128], ident[:])
+                nc.tensor.transpose(tp[:, 128 * t : 128 * t + 128], ca_f[b // 2][:, t, 128 * (b % 2) : 128 * (b % 2) + 128], ident[:])
             c0_psum[b] = tp[:].bitcast(BF16).rearrange("p (n e) -> p e n", e=2)
 
         def c0_prep_b():
@@ -191,7 +198,7 @@ def tile_odelstmcell_pa_kernel(tc, inputs, h0, c0, w_ih, w_hh, b_ih, b_hh, out_0
             for k in range(3):
                 tp = psum.tile([P, 2, 2, P], F32, tag="bank")
                 for i in range(2):
-                    e, s = divmod(2 * k + i, 3)
+                    e, s = (i, 0) if k == 0 else (k - 1, 1 + i)
                     for u in range(2):
                         if s == 0:
                             src = wih_f[:, e, 128 * u : 128 * u + 128]
@@ -224,7 +231,7 @@ def tile_odelstmcell_pa_kernel(tc, inputs, h0, c0, w_ih, w_hh, b_ih, b_hh, out_0
             q = 4 * b + GATE_ORDER.index(gi)
             n = (NA, P)[part]
             for s in which:
-                col = (q * 6 + e * 3 + s) * P
+                col = (q * 6 + (e if s == 0 else 1 + 2 * e + s)) * P
                 if s == 0 or cell == 0:
                     rc, rs, off = (aA_codes, aB_codes)[part], (aA_scales, aB_scales)[part], s * n
                 else:
@@ -335,7 +342,9 @@ def tile_odelstmcell_pa_kernel(tc, inputs, h0, c0, w_ih, w_hh, b_ih, b_hh, out_0
             for n in new:
                 if n + RAW_BUFS < BLOCKS:
                     load_block(n + RAW_BUFS)
-                if n + RAW_BUFS == 11:
+                if n + RAW_BUFS == 10:
+                    load_ca(1)
+                if n + RAW_BUFS == 13:
                     load_b()
             ops = [step_of(q) for q in old]
             for i, n in enumerate(new):
@@ -355,7 +364,7 @@ def tile_odelstmcell_pa_kernel(tc, inputs, h0, c0, w_ih, w_hh, b_ih, b_hh, out_0
                 for e in range(2):
                     passes(gt[:, e, :], 2 * b + e, GATE_ORDER[o], 0, 0)
                 pair_act(b, GATE_ORDER[o], 0, [gt[:, e, :] for e in range(2)])
-            if 9 in old:
+            if 11 in old:
                 acts_b_prep()
             if 11 in old:
                 c0_prep_b()

@@ -18,7 +18,7 @@ UNITS = 8
 PAIRS = 4
 BLOCKS = 16
 FLOPS = 2 * 2 * 384 * 4096 * 1536
-RAW_BUFS = 8
+RAW_BUFS = 7
 OUTPUTS_AFTER = {3: (1,), 5: (2, 3, 4)}
 VECTOR_AFTER = {1: (0,)}
 GATE_ORDER = (1, 0, 2, 3)
@@ -69,15 +69,6 @@ def tile_odelstmcell_pa_kernel(tc, inputs, h0, c0, w_ih, w_hh, b_ih, b_hh, out_0
         whh_v = w_hh.rearrange("(g b p e) k -> b g p (e k)", g=4, b=4, p=P, e=2)
         raw_views = {}
 
-        def load_b():
-            nc.sync.dma_start(out=xb_raw[:], in_=rows_b(inputs))
-            nc.sync.dma_start(out=hb_raw[:], in_=rows_b(h0))
-            nc.sync.dma_start(out=cb_raw[:], in_=rows_b(c0))
-
-        def load_ca(half):
-            lo = 512 * half
-            nc.sync.dma_start(out=(ca0_raw, ca1_raw)[half][:], in_=rows_a(c0)[:, :, lo : lo + 512])
-
         def load_block(q):
             b, o = divmod(q, 4)
             gi = GATE_ORDER[o]
@@ -95,14 +86,27 @@ def tile_odelstmcell_pa_kernel(tc, inputs, h0, c0, w_ih, w_hh, b_ih, b_hh, out_0
                 whh_raw[:].bitcast(F32).rearrange("p (e w) -> p e w", e=2),
             )
 
-        nc.sync.dma_start(out=xa_raw[:], in_=rows_a(inputs))
-        nc.sync.dma_start(out=ha_raw[:], in_=rows_a(h0))
-        for q in range(RAW_BUFS):
-            load_block(q)
-            if q == 7:
-                load_ca(0)
-            if q == 13:
-                load_b()
+        others = {
+            "xA": (xa_raw[:], rows_a(inputs)),
+            "hA": (ha_raw[:], rows_a(h0)),
+            "cA0": (ca0_raw[:], rows_a(c0)[:, :, 0:512]),
+            "cA1": (ca1_raw[:], rows_a(c0)[:, :, 512:1024]),
+            "xB": (xb_raw[:], rows_b(inputs)),
+            "hB": (hb_raw[:], rows_b(h0)),
+            "cB": (cb_raw[:], rows_b(c0)),
+        }
+        to_load = ["xA","hA",0,1,2,"xB","hB",3,4,5,6,7,"cA0",8,9,10,11,"cA1",12,13,"cB",14,15]
+
+        def issue_loads(last):
+            while to_load and (to_load[0] in others or to_load[0] <= last):
+                item = to_load.pop(0)
+                if item in others:
+                    tile, src = others[item]
+                    nc.sync.dma_start(out=tile, in_=src)
+                else:
+                    load_block(item)
+
+        issue_loads(RAW_BUFS - 1)
         xa_f = xa_raw[:].rearrange("p t k -> p (t k)").bitcast(F32).rearrange("p (t w) -> p t w", t=2)
         ha_f = ha_raw[:].rearrange("p t k -> p (t k)").bitcast(F32).rearrange("p (t w) -> p t w", t=2)
         ca_f = [
@@ -151,7 +155,7 @@ def tile_odelstmcell_pa_kernel(tc, inputs, h0, c0, w_ih, w_hh, b_ih, b_hh, out_0
                         lo = 256 * (s - 1) + 128 * u
                         src = ha_f[:, t, lo : lo + 128]
                     nc.tensor.transpose(tp[:, t, u, :], src, ident[:])
-            evac("VSS"[s], aA_grp5[:, s], tp[:].rearrange("p t u m -> p t m u"))
+            evac("VSV"[s], aA_grp5[:, s], tp[:].rearrange("p t u m -> p t m u"))
         for s in range(3):
             quantise(aA_codes, aA_scales, aA_grp[:].bitcast(BF16), s * NA, (s + 1) * NA)
 
@@ -161,8 +165,6 @@ def tile_odelstmcell_pa_kernel(tc, inputs, h0, c0, w_ih, w_hh, b_ih, b_hh, out_0
             nc.vector.tensor_copy(out=bias_w[:], in_=tp[:, 0, 0, 0:32])
             bias_wb = bias_w[:].bitcast(BF16)
             nc.vector.tensor_tensor(out=bias[:], in0=bias_wb[:, 0:32], in1=bias_wb[:, 32:64], op=ALU.add)
-
-        bias_prep()
 
         def acts_b_prep():
             aB_grp4 = aB_grp[:].rearrange("p (s m u) -> p s m u", s=3, u=2)
@@ -260,7 +262,7 @@ def tile_odelstmcell_pa_kernel(tc, inputs, h0, c0, w_ih, w_hh, b_ih, b_hh, out_0
             return slice(0, NA) if part == 0 else slice(NA, NB)
 
         def pair_act(b, gi, part, banks):
-            a = gact.tile([P, 2, (NA, P)[part]], F32, tag="g%d" % gi, bufs=(3, 3, 3, 4)[gi])
+            a = gact.tile([P, 2, (NA, P)[part]], F32, tag=("g%d", "b%d")[part] % gi, bufs=((3, 3, 3, 4), (2, 2, 2, 3))[part][gi])
             for e in range(2):
                 act(a[:, e, :], banks[e], gi, 2 * b + e)
             pa[(b, gi, part)] = a
@@ -282,13 +284,23 @@ def tile_odelstmcell_pa_kernel(tc, inputs, h0, c0, w_ih, w_hh, b_ih, b_hh, out_0
                 out=c_st[part][:, 2 * b : 2 * b + 2, :], in0=pa[(b, 1, part)][:], in1=pa[(b, 0, part)][:], op=ALU.add
             )
 
+        def pair_ig_units(b, part):
+            for e in range(2):
+                i = pa[(b, 0, part)][:, e, :]
+                mult(i, i, pa[(b, 2, part)][:, e, :])
+
+        def pair_add_units(b, part):
+            for e in range(2):
+                nc.vector.tensor_tensor(
+                    out=c_st[part][:, 2 * b + e, :],
+                    in0=pa[(b, 1, part)][:, e, :],
+                    in1=pa[(b, 0, part)][:, e, :],
+                    op=ALU.add,
+                )
+
         def pair_ig_add(b, part):
-            f, i, g = (pa[(b, x, part)] for x in (1, 0, 2))
-            for e in range(2):
-                mult(i[:, e, :], i[:, e, :], g[:, e, :])
-            for e in range(2):
-                c = c_st[part][:, 2 * b + e, :]
-                nc.vector.tensor_tensor(out=c, in0=f[:, e, :], in1=i[:, e, :], op=ALU.add)
+            pair_ig_units(b, part)
+            pair_add_units(b, part)
 
         def pair_tanh(b, part):
             nc.scalar.activation(
@@ -299,82 +311,95 @@ def tile_odelstmcell_pa_kernel(tc, inputs, h0, c0, w_ih, w_hh, b_ih, b_hh, out_0
             t = 2 * (b % 2)
             mult(h1_pl[:, b // 2, t : t + 2, cols(part)], pa[(b, 3, part)][:], pa[(b, 2, part)][:])
 
-        def h1_quant(g, part):
-            n = (NA, P)[part]
+        def h1_interleave(g, part):
             grp = (hA_grp, hB_grp)[part]
             nc.vector.tensor_copy(out=grp[:, g], in_=h1_pl[:, g, :, cols(part)].rearrange("p t n -> p n t"))
+
+        def h1_quantise(g, part):
+            n = (NA, P)[part]
             quantise(
                 (hA_codes, hB_codes)[part],
                 (hA_scales, hB_scales)[part],
-                grp[:].rearrange("p g n t -> p (g n t)"),
+                (hA_grp, hB_grp)[part][:].rearrange("p g n t -> p (g n t)"),
                 g * n,
                 (g + 1) * n,
             )
 
-        runs = [((0, 1), (0,)), ((2,), (1,)), ((3,), (2,)), ((4, 5), (3,))]
-        runs += [((n, n + 1), (n - 2, n - 1)) for n in range(6, BLOCKS, 2)]
-        runs.append(((), (BLOCKS - 2, BLOCKS - 1)))
+        def b_half(b, half):
+            bank = psum.tile([P, 4, P], F32, tag="bank")
+            for l in range(2):
+                gi = GATE_ORDER[2 * half + l]
+                for e in range(2):
+                    passes(bank[:, 2 * l + e, :], 2 * b + e, gi, 0, 1)
+            for l in range(2):
+                pair_act(b, GATE_ORDER[2 * half + l], 1, [bank[:, 2 * l + e, :] for e in range(2)])
 
-        def step_of(q):
-            b, o = divmod(q, 4)
-            if o == 0 and b > 0:
-                return lambda: pair_ig(b - 1, 0)
-            if o == 1 and b > 0:
-                if b == 1:
-                    return lambda: (pair_fc(0, 0, 0), pair_add(0, 0))
-                return lambda: pair_add(b - 1, 0)
-            if o == 2 and b > 0:
-                return lambda: pair_fc(b, 0, 0)
-            if o == 3 and b > 0:
-                return lambda: pair_h(b - 1, 0)
-            return lambda: None
+        steps_by_name = {"fc": lambda b, part: pair_fc(b, part, 0), "ig": pair_ig, "add": pair_add, "h": pair_h, "tanh": pair_tanh, "hc": h1_interleave, "hq": h1_quantise, "igadd": pair_ig_add}
+        ops = {4:[["ig",0,0]],5:[["fc",0,0],["add",0,0]],6:[["fc",1,0]],7:[["h",0,0]],8:[["ig",1,0]],9:[["add",1,0]],10:[["fc",2,0]],11:[["h",1,0]],12:[["ig",2,0]],13:[["add",2,0],["fc",0,1],["ig",0,1]],14:[["fc",3,0],["hc",0,0],["h",2,0],["hq",0,0],["add",0,1]],15:[]}
+        tanhs = {6:[[0,0]],10:[[1,0]],14:[[2,0]]}
+        runs = [[[0,1],[0],[]],[[2],[1],[["actsB"]]],[[3],[2],[["half",0,0]]],[[4,5],[3],[["half",0,1]]],[[6,7],[4,5],[["c0A",0],["c0A",1]]],[[8,9],[6,7],[]],[[10,11],[8,9],[["c0A",2]]],[[12,13],[10,11],[["c0B"]]],[[14,15],[12,13],[["c0A",3]]],[[],[14,15],[["before",15,1,0]]]]
 
-        for new, old in runs:
+        def do_ops(q):
+            for name, b, part in ops.get(q, ()):
+                steps_by_name[name](b, part)
+
+        for new, old, post in runs:
             banks = {}
             for n in new:
                 banks[n] = transposes(n)
+            for item in post:
+                if item[0] == "c0A":
+                    c0_prep_a(item[1])
             for q in old:
-                if q % 4 == 1 and q > 1 or q == 4:
-                    c0_prep_a(0 if q == 4 else q // 4)
-            for q in old:
-                if q % 4 == 2 and q > 4:
-                    pair_tanh(q // 4 - 1, 0)
+                for b, part in tanhs.get(q, ()):
+                    pair_tanh(b, part)
             for n in new:
-                if n + RAW_BUFS < BLOCKS:
-                    load_block(n + RAW_BUFS)
-                if n + RAW_BUFS == 10:
-                    load_ca(1)
-                if n + RAW_BUFS == 13:
-                    load_b()
-            ops = [step_of(q) for q in old]
+                issue_loads(n + RAW_BUFS)
             for i, n in enumerate(new):
                 grp = grpp.tile([P, 6 * 2 * P], F32, tag="grp", align_bytes=64)
                 for k in range(3):
-                    evac_bank("V" if k == 1 and n % 2 == 0 else "S", grp, k, banks[n][k])
-                if i < len(ops):
-                    ops[i]()
+                    evac_bank("V" if k == 1 and n % 4 != 3 else "S", grp, k, banks[n][k])
+                if i < len(old):
+                    do_ops(old[i])
                 quantise_block(n, grp)
-            for i in range(len(new), len(ops)):
-                ops[i]()
-            if 12 in old:
-                h1_quant(0, 0)
+                if n == 0:
+                    bias_prep()
+            for i in range(len(new), len(old)):
+                do_ops(old[i])
             for q in old:
                 b, o = divmod(q, 4)
+                for item in post:
+                    if item[0] == "before" and item[1] == q:
+                        b_half(item[2], item[3])
                 gt = psum.tile([P, 2, NA], F32, tag="bank")
                 for e in range(2):
                     passes(gt[:, e, :], 2 * b + e, GATE_ORDER[o], 0, 0)
                 pair_act(b, GATE_ORDER[o], 0, [gt[:, e, :] for e in range(2)])
-            if 11 in old:
-                acts_b_prep()
-            if 11 in old:
-                c0_prep_b()
-        pair_ig(PAIRS - 1, 0)
-        pair_add(PAIRS - 1, 0)
+            for item in post:
+                if item[0] == "actsB":
+                    acts_b_prep()
+                elif item[0] == "c0B":
+                    c0_prep_b()
+                elif item[0] == "half":
+                    b_half(item[1], item[2])
+        for name, b, part in [["igadd",3,0],["tanh",0,1],["h",0,1]]:
+            steps_by_name[name](b, part)
 
         def gate_mx(b, part, cell):
             n = (NA, P)[part]
             out = {}
             gates_per_bank = 512 // (2 * n)
+            if cell == 1 and b == 0 and part == 0:
+                banks = []
+                for o in range(4):
+                    bank = psum.tile([P, 2, n], F32, tag="bank")
+                    passes(bank[:, 0, :], 2 * b, GATE_ORDER[o], cell, part, (0, 1))
+                    banks.append(bank)
+                for o in range(4):
+                    passes(banks[o][:, 0, :], 2 * b, GATE_ORDER[o], cell, part, (2,))
+                    passes(banks[o][:, 1, :], 2 * b + 1, GATE_ORDER[o], cell, part)
+                    out[GATE_ORDER[o]] = [banks[o][:, e, :] for e in range(2)]
+                return out
             for g0 in range(0, 4, gates_per_bank):
                 bank = psum.tile([P, 2 * gates_per_bank, n], F32, tag="bank")
                 for l in range(gates_per_bank):
@@ -384,28 +409,33 @@ def tile_odelstmcell_pa_kernel(tc, inputs, h0, c0, w_ih, w_hh, b_ih, b_hh, out_0
                     out[gi] = [bank[:, 2 * l + e, :] for e in range(2)]
             return out
 
-        for b in range(PAIRS):
-            gt = gate_mx(b, 1, 0)
-            pair_act(b, 1, 1, gt[1])
-            pair_act(b, 0, 1, gt[0])
-            if b == 0:
+        for b in range(1, PAIRS):
+            if (b, 0) not in ((1, 0),):
+                b_half(b, 0)
+            if b == 1:
                 pair_tanh(PAIRS - 1, 0)
             pair_fc(b, 1, 0)
-            if b == 0:
+            if b == PAIRS - 1:
+                h1_quantise(0, 1)
+            if b == 1:
                 pair_h(PAIRS - 1, 0)
-            pair_act(b, 2, 1, gt[2])
-            pair_act(b, 3, 1, gt[3])
-            pair_ig_add(b, 1)
-            if b == 0:
-                h1_quant(1, 0)
-            if b > 0:
+            if (b, 1) not in ((1, 0),):
+                b_half(b, 1)
+            pair_ig_units(b, 1)
+            if b == 1:
+                h1_interleave(1, 0)
+            if b > 1:
                 pair_tanh(b - 1, 1)
                 pair_h(b - 1, 1)
+            pair_add_units(b, 1)
+            if b == 1:
+                h1_quantise(1, 0)
             if b == 2:
-                h1_quant(0, 1)
+                h1_interleave(0, 1)
         pair_tanh(PAIRS - 1, 1)
         pair_h(PAIRS - 1, 1)
-        h1_quant(1, 1)
+        h1_interleave(1, 1)
+        h1_quantise(1, 1)
 
         def output_transposes(b, part):
             nt = 2 - part

@@ -337,7 +337,7 @@ def tile_odelstmcell_pa_kernel(tc, inputs, h0, c0, w_ih, w_hh, b_ih, b_hh, out_0
         steps_by_name = {"fc": lambda b, part: pair_fc(b, part, 0), "ig": pair_ig, "add": pair_add, "h": pair_h, "tanh": pair_tanh, "hc": h1_interleave, "hq": h1_quantise, "igadd": pair_ig_add}
         ops = {4:[["ig",0,0]],5:[["fc",0,0],["add",0,0]],6:[["fc",1,0]],7:[["h",0,0]],8:[["ig",1,0]],9:[["add",1,0]],10:[["fc",2,0]],11:[["h",1,0]],12:[["ig",2,0]],13:[["add",2,0],["fc",0,1],["ig",0,1]],14:[["fc",3,0],["hc",0,0],["h",2,0],["hq",0,0],["add",0,1]],15:[]}
         tanhs = {6:[[0,0]],10:[[1,0]],14:[[2,0]]}
-        runs = [[[0,1],[0],[]],[[2],[1],[["actsB"]]],[[3],[2],[["half",0,0]]],[[4,5],[3],[["half",0,1]]],[[6,7],[4,5],[["c0A",0],["c0A",1]]],[[8,9],[6,7],[]],[[10,11],[8,9],[["c0A",2]]],[[12,13],[10,11],[["c0B"]]],[[14,15],[12,13],[["c0A",3]]],[[],[14,15],[["before",15,1,0]]]]
+        runs = [[[0,1],[0],[]],[[2],[1],[["actsB"]]],[[3],[2],[["half",0,0]]],[[4,5],[3],[["half",0,1]]],[[6,7],[4,5],[["c0A",0],["c0A",1]]],[[8,9],[6,7],[]],[[10,11],[8,9],[["c0A",2]]],[[12],[10],[]],[[13],[11],[["c0B"]]],[[14],[12],[]],[[15],[13],[["c0A",3]]],[[],[14,15],[["before",15,1,0]]]]
 
         def do_ops(q):
             for name, b, part in ops.get(q, ()):

from contextlib import ExitStack

import concourse.mybir as mybir
from concourse.masks import make_identity

F32 = mybir.dt.float32
BF16 = mybir.dt.bfloat16
U32 = mybir.dt.uint32
U8 = mybir.dt.uint8
FP8X4 = mybir.dt.float8_e4m3fn_x4
ACT = mybir.ActivationFunctionType
ALU = mybir.AluOpType

P = 128
NB = 384
NA = 256
UNITS = 8
PAIRS = 4
BLOCKS = 16
FLOPS = 2 * 2 * 384 * 4096 * 1536
RAW_BUFS = 7
OUTPUTS_AFTER = {3: (1,), 5: (2, 3, 4)}
VECTOR_AFTER = {1: (0,)}
GATE_ORDER = (1, 0, 2, 3)
GATE_FUNC = (ACT.Sigmoid, ACT.Sigmoid, ACT.Tanh, ACT.Sigmoid)


def tile_odelstmcell_pa_kernel(tc, inputs, h0, c0, w_ih, w_hh, b_ih, b_hh, out_0, out_1):
    nc = tc.nc
    with ExitStack() as ctx:
        const = ctx.enter_context(tc.tile_pool(name="const", bufs=1))
        rawp = ctx.enter_context(tc.tile_pool(name="rawp", bufs=RAW_BUFS))
        grpp = ctx.enter_context(tc.tile_pool(name="grpp", bufs=3))
        gact = ctx.enter_context(tc.tile_pool(name="gact", bufs=3))
        outp = ctx.enter_context(tc.tile_pool(name="outp", bufs=2))
        psum = ctx.enter_context(tc.psum_pool(name="psum", bufs=8))
        ctx.enter_context(tc.manual_schedule())

        def evac(who, out, in_):
            if who == "S":
                nc.scalar.copy(out=out, in_=in_)
            else:
                nc.vector.tensor_copy(out=out, in_=in_)

        bias_raw = const.tile([P, 256], BF16)
        nc.vector.memset(bias_raw[:], 0.0)
        nc.scalar.dma_start(out=bias_raw[0:16, :], in_=b_ih.rearrange("(r c) -> r c", c=256))
        nc.scalar.dma_start(out=bias_raw[16:32, :], in_=b_hh.rearrange("(r c) -> r c", c=256))
        warm = const.tile([P, 1], F32)
        nc.vector.memset(warm[:], 0.0)
        nc.scalar.activation(out=warm[:], in_=warm[:], func=ACT.Sigmoid)
        ident = const.tile([P, P], F32)
        make_identity(nc, ident[:])

        def rows_a(x):
            return x[0:NA, :].rearrange("(p t) k -> p t k", t=2)

        def rows_b(x):
            return x[NA:NB, :]

        xa_raw = const.tile([P, 2, 512], BF16)
        ha_raw = const.tile([P, 2, 1024], BF16)
        ca0_raw = const.tile([P, 2, 512], BF16)
        ca1_raw = const.tile([P, 2, 512], BF16)
        xb_raw = const.tile([P, 512], BF16)
        hb_raw = const.tile([P, 1024], BF16)
        cb_raw = const.tile([P, 1024], BF16)
        wih_v = w_ih.rearrange("(g b p e) k -> b g p (e k)", g=4, b=4, p=P, e=2)
        whh_v = w_hh.rearrange("(g b p e) k -> b g p (e k)", g=4, b=4, p=P, e=2)
        raw_views = {}

        def load_block(q):
            b, o = divmod(q, 4)
            gi = GATE_ORDER[o]
            wih_raw = rawp.tile([P, 2 * 512], BF16, tag="wih", align_bytes=64)
            nc.sync.dma_start(out=wih_raw[:], in_=wih_v[b, gi])
            whh_raw = rawp.tile([P, 2 * 1024], BF16, tag="whh")
            parts = 2 if q < 2 else 1
            width = 2 * 1024 // parts
            for i in range(parts):
                nc.sync.dma_start(
                    out=whh_raw[:, i * width : (i + 1) * width], in_=whh_v[b, gi][:, i * width : (i + 1) * width]
                )
            raw_views[q] = (
                wih_raw[:].bitcast(F32).rearrange("p (e w) -> p e w", e=2),
                whh_raw[:].bitcast(F32).rearrange("p (e w) -> p e w", e=2),
            )

        others = {
            "xA": (xa_raw[:], rows_a(inputs)),
            "hA": (ha_raw[:], rows_a(h0)),
            "cA0": (ca0_raw[:], rows_a(c0)[:, :, 0:512]),
            "cA1": (ca1_raw[:], rows_a(c0)[:, :, 512:1024]),
            "xB": (xb_raw[:], rows_b(inputs)),
            "hB": (hb_raw[:], rows_b(h0)),
            "cB": (cb_raw[:], rows_b(c0)),
        }
        to_load = ["xA","hA",0,1,2,"xB","hB",3,4,5,6,7,"cA0",8,9,10,11,"cA1",12,13,"cB",14,15]

        def issue_loads(last):
            while to_load and (to_load[0] in others or to_load[0] <= last):
                item = to_load.pop(0)
                if item in others:
                    tile, src = others[item]
                    nc.sync.dma_start(out=tile, in_=src)
                else:
                    load_block(item)

        issue_loads(RAW_BUFS - 1)
        xa_f = xa_raw[:].rearrange("p t k -> p (t k)").bitcast(F32).rearrange("p (t w) -> p t w", t=2)
        ha_f = ha_raw[:].rearrange("p t k -> p (t k)").bitcast(F32).rearrange("p (t w) -> p t w", t=2)
        ca_f = [
            raw[:].rearrange("p t k -> p (t k)").bitcast(F32).rearrange("p (t w) -> p t w", t=2) for raw in (ca0_raw, ca1_raw)
        ]
        xb_f = xb_raw[:].bitcast(F32)
        hb_f = hb_raw[:].bitcast(F32)
        cb_f = cb_raw[:].bitcast(F32)

        aA_grp = const.tile([P, 3 * NA * 2], F32, align_bytes=64)
        aB_grp = const.tile([P, 3 * P * 2], F32, align_bytes=64)
        aA_codes = const.tile([P, 3 * NA], U32, align_bytes=64)
        aA_scales = const.tile([P, 3 * NA], U8, align_bytes=64)
        aB_codes = const.tile([P, 3 * P], U32, align_bytes=64)
        aB_scales = const.tile([P, 3 * P], U8, align_bytes=64)
        h1_pl = const.tile([P, 2, 4, NB], BF16)
        hA_grp = const.tile([P, 2, NA, 4], BF16, align_bytes=64)
        hB_grp = const.tile([P, 2, P, 4], BF16, align_bytes=64)
        hA_codes = const.tile([P, 2 * NA], U32, align_bytes=64)
        hA_scales = const.tile([P, 2 * NA], U8, align_bytes=64)
        hB_codes = const.tile([P, 2 * P], U32, align_bytes=64)
        hB_scales = const.tile([P, 2 * P], U8, align_bytes=64)
        c0B = const.tile([P, PAIRS * P], F32)
        c0B_bf = c0B[:].bitcast(BF16).rearrange("p (b n e) -> p b e n", b=PAIRS, e=2)
        cA_st = const.tile([P, UNITS, NA], F32, align_bytes=64)
        cB_st = const.tile([P, UNITS, P], F32, align_bytes=64)
        c_st = (cA_st, cB_st)
        w_codes = const.tile([P, 96 * P], U32, align_bytes=64)
        w_scales = const.tile([P, 96 * P], U8, align_bytes=64)
        bias_w = const.tile([P, 32], F32)
        bias = const.tile([P, 32], F32)

        def quantise(codes, scales, grp_bf, lo, hi):
            nc.vector.quantize_mx(
                out=codes[:, lo:hi].bitcast(FP8X4), scales=scales[:, lo:hi], in_=grp_bf[:, 4 * lo : 4 * hi]
            )

        aA_grp5 = aA_grp[:].rearrange("p (s t m u) -> p s t m u", s=3, t=2, u=2)
        for s in range(3):
            tp = psum.tile([P, 2, 2, P], F32, tag="bank")
            for t in range(2):
                for u in range(2):
                    if s == 0:
                        src = xa_f[:, t, 128 * u : 128 * u + 128]
                    else:
                        lo = 256 * (s - 1) + 128 * u
                        src = ha_f[:, t, lo : lo + 128]
                    nc.tensor.transpose(tp[:, t, u, :], src, ident[:])
            evac("VSV"[s], aA_grp5[:, s], tp[:].rearrange("p t u m -> p t m u"))
        for s in range(3):
            quantise(aA_codes, aA_scales, aA_grp[:].bitcast(BF16), s * NA, (s + 1) * NA)

        def bias_prep():
            tp = psum.tile([P, 2, 2, P], F32, tag="bank")
            nc.tensor.transpose(tp[:, 0, 0, :], bias_raw[:].bitcast(F32), ident[:])
            nc.vector.tensor_copy(out=bias_w[:], in_=tp[:, 0, 0, 0:32])
            bias_wb = bias_w[:].bitcast(BF16)
            nc.vector.tensor_tensor(out=bias[:], in0=bias_wb[:, 0:32], in1=bias_wb[:, 32:64], op=ALU.add)

        def acts_b_prep():
            aB_grp4 = aB_grp[:].rearrange("p (s m u) -> p s m u", s=3, u=2)
            for s0, ns in ((0, 2), (2, 1)):
                tp = psum.tile([P, 2, 2, P], F32, tag="bank")
                for sl in range(ns):
                    s = s0 + sl
                    for u in range(2):
                        lo = 256 * (s - 1) + 128 * u
                        src = xb_f[:, 128 * u : 128 * u + 128] if s == 0 else hb_f[:, lo : lo + 128]
                        nc.tensor.transpose(tp[:, sl, u, :], src, ident[:])
                evac("VS"[s0 // 2], aB_grp4[:, s0 : s0 + ns], tp[:, 0:ns].rearrange("p s u m -> p s m u"))
            quantise(aB_codes, aB_scales, aB_grp[:].bitcast(BF16), 0, 2 * P)
            quantise(aB_codes, aB_scales, aB_grp[:].bitcast(BF16), 2 * P, 3 * P)

        c0_psum = {}

        def c0_prep_a(b):
            tp = psum.tile([P, NA], F32, tag="bank")
            for t in range(2):
                nc.tensor.transpose(tp[:, 128 * t : 128 * t + 128], ca_f[b // 2][:, t, 128 * (b % 2) : 128 * (b % 2) + 128], ident[:])
            c0_psum[b] = tp[:].bitcast(BF16).rearrange("p (n e) -> p e n", e=2)

        def c0_prep_b():
            tp = psum.tile([P, PAIRS * P], F32, tag="bank")
            for b in range(PAIRS):
                nc.tensor.transpose(tp[:, 128 * b : 128 * b + 128], cb_f[:, 128 * b : 128 * b + 128], ident[:])
            evac("S", c0B[:], tp[:])

        def transposes(q):
            wih_f, whh_f = raw_views[q]
            banks = []
            for k in range(3):
                tp = psum.tile([P, 2, 2, P], F32, tag="bank")
                for i in range(2):
                    e, s = (i, 0) if k == 0 else (k - 1, 1 + i)
                    for u in range(2):
                        if s == 0:
                            src = wih_f[:, e, 128 * u : 128 * u + 128]
                        else:
                            lo = 256 * (s - 1) + 128 * u
                            src = whh_f[:, e, lo : lo + 128]
                        nc.tensor.transpose(tp[:, i, u, :], src, ident[:])
                banks.append(tp)
            return banks

        def evac_bank(who, grp, k, bank):
            evac(
                who,
                grp[:, 512 * k : 512 * k + 512].rearrange("p (i m u) -> p i m u", i=2, u=2),
                bank[:].rearrange("p i u m -> p i m u"),
            )

        def quantise_block(q, grp):
            grp_bf = grp[:].bitcast(BF16)
            for lo, hi in ((0, 4 * P), (4 * P, 6 * P)):
                base = q * 6 * P
                nc.vector.quantize_mx(
                    out=w_codes[:, base + lo : base + hi].bitcast(FP8X4),
                    scales=w_scales[:, base + lo : base + hi],
                    in_=grp_bf[:, 4 * lo : 4 * hi],
                )

        def passes(out, j, gi, cell, part, which=(0, 1, 2)):
            b, e = divmod(j, 2)
            q = 4 * b + GATE_ORDER.index(gi)
            n = (NA, P)[part]
            for s in which:
                col = (q * 6 + (e if s == 0 else 1 + 2 * e + s)) * P
                if s == 0 or cell == 0:
                    rc, rs, off = (aA_codes, aB_codes)[part], (aA_scales, aB_scales)[part], s * n
                else:
                    rc, rs, off = (hA_codes, hB_codes)[part], (hA_scales, hB_scales)[part], (s - 1) * n
                nc.tensor.matmul_mx(
                    out=out,
                    lhsT=w_codes[:, col : col + P].bitcast(FP8X4),
                    lhsT_scale=w_scales[:, col : col + P],
                    rhs=rc[:, off : off + n].bitcast(FP8X4),
                    rhs_scale=rs[:, off : off + n],
                    start=(s == 0),
                    stop=(s == 2),
                )

        def act(out, in_, gi, j):
            nc.scalar.activation(
                out=out, in_=in_, func=GATE_FUNC[gi], bias=bias[:, 8 * gi + j : 8 * gi + j + 1]
            )

        def mult(out, in0, in1):
            nc.vector.tensor_tensor(out=out, in0=in0, in1=in1, op=ALU.mult)

        pa = {}

        def cols(part):
            return slice(0, NA) if part == 0 else slice(NA, NB)

        def pair_act(b, gi, part, banks):
            a = gact.tile([P, 2, (NA, P)[part]], F32, tag=("g%d", "b%d")[part] % gi, bufs=((3, 3, 3, 4), (2, 2, 2, 3))[part][gi])
            for e in range(2):
                act(a[:, e, :], banks[e], gi, 2 * b + e)
            pa[(b, gi, part)] = a

        def pair_fc(b, part, cell):
            a = pa[(b, 1, part)]
            if cell == 1:
                c = c_st[part][:, 2 * b : 2 * b + 2, :]
            else:
                c = c0_psum[b] if part == 0 else c0B_bf[:, b]
            mult(a[:], a[:], c)

        def pair_ig(b, part):
            a = pa[(b, 0, part)]
            mult(a[:], a[:], pa[(b, 2, part)][:])

        def pair_add(b, part):
            nc.vector.tensor_tensor(
                out=c_st[part][:, 2 * b : 2 * b + 2, :], in0=pa[(b, 1, part)][:], in1=pa[(b, 0, part)][:], op=ALU.add
            )

        def pair_ig_units(b, part):
            for e in range(2):
                i = pa[(b, 0, part)][:, e, :]
                mult(i, i, pa[(b, 2, part)][:, e, :])

        def pair_add_units(b, part):
            for e in range(2):
                nc.vector.tensor_tensor(
                    out=c_st[part][:, 2 * b + e, :],
                    in0=pa[(b, 1, part)][:, e, :],
                    in1=pa[(b, 0, part)][:, e, :],
                    op=ALU.add,
                )

        def pair_ig_add(b, part):
            pair_ig_units(b, part)
            pair_add_units(b, part)

        def pair_tanh(b, part):
            nc.scalar.activation(
                out=pa[(b, 2, part)][:], in_=c_st[part][:, 2 * b : 2 * b + 2, :], func=ACT.Tanh
            )

        def pair_h(b, part):
            t = 2 * (b % 2)
            mult(h1_pl[:, b // 2, t : t + 2, cols(part)], pa[(b, 3, part)][:], pa[(b, 2, part)][:])

        def h1_interleave(g, part):
            grp = (hA_grp, hB_grp)[part]
            nc.vector.tensor_copy(out=grp[:, g], in_=h1_pl[:, g, :, cols(part)].rearrange("p t n -> p n t"))

        def h1_quantise(g, part):
            n = (NA, P)[part]
            quantise(
                (hA_codes, hB_codes)[part],
                (hA_scales, hB_scales)[part],
                (hA_grp, hB_grp)[part][:].rearrange("p g n t -> p (g n t)"),
                g * n,
                (g + 1) * n,
            )

        def b_half(b, half):
            bank = psum.tile([P, 4, P], F32, tag="bank")
            for l in range(2):
                gi = GATE_ORDER[2 * half + l]
                for e in range(2):
                    passes(bank[:, 2 * l + e, :], 2 * b + e, gi, 0, 1)
            for l in range(2):
                pair_act(b, GATE_ORDER[2 * half + l], 1, [bank[:, 2 * l + e, :] for e in range(2)])

        steps_by_name = {"fc": lambda b, part: pair_fc(b, part, 0), "ig": pair_ig, "add": pair_add, "h": pair_h, "tanh": pair_tanh, "hc": h1_interleave, "hq": h1_quantise, "igadd": pair_ig_add}
        ops = {4:[["ig",0,0]],5:[["fc",0,0],["add",0,0]],6:[["fc",1,0]],7:[["h",0,0]],8:[["ig",1,0]],9:[["add",1,0]],10:[["fc",2,0]],11:[["h",1,0]],12:[["ig",2,0]],13:[["add",2,0],["fc",0,1],["ig",0,1]],14:[["fc",3,0],["hc",0,0],["h",2,0],["hq",0,0],["add",0,1]],15:[]}
        tanhs = {6:[[0,0]],10:[[1,0]],14:[[2,0]]}
        runs = [[[0,1],[0],[]],[[2],[1],[["actsB"]]],[[3],[2],[["half",0,0]]],[[4,5],[3],[["half",0,1]]],[[6,7],[4,5],[["c0A",0],["c0A",1]]],[[8,9],[6,7],[]],[[10,11],[8,9],[["c0A",2]]],[[12],[10],[]],[[13],[11],[["c0B"]]],[[14],[12],[]],[[15],[13],[["c0A",3]]],[[],[14,15],[["before",15,1,0]]]]

        def do_ops(q):
            for name, b, part in ops.get(q, ()):
                steps_by_name[name](b, part)

        for new, old, post in runs:
            banks = {}
            for n in new:
                banks[n] = transposes(n)
            for item in post:
                if item[0] == "c0A":
                    c0_prep_a(item[1])
            for q in old:
                for b, part in tanhs.get(q, ()):
                    pair_tanh(b, part)
            for n in new:
                issue_loads(n + RAW_BUFS)
            for i, n in enumerate(new):
                grp = grpp.tile([P, 6 * 2 * P], F32, tag="grp", align_bytes=64)
                for k in range(3):
                    evac_bank("V" if k == 1 and n % 4 != 3 else "S", grp, k, banks[n][k])
                if i < len(old):
                    do_ops(old[i])
                quantise_block(n, grp)
                if n == 0:
                    bias_prep()
            for i in range(len(new), len(old)):
                do_ops(old[i])
            for q in old:
                b, o = divmod(q, 4)
                for item in post:
                    if item[0] == "before" and item[1] == q:
                        b_half(item[2], item[3])
                gt = psum.tile([P, 2, NA], F32, tag="bank")
                for e in range(2):
                    passes(gt[:, e, :], 2 * b + e, GATE_ORDER[o], 0, 0)
                pair_act(b, GATE_ORDER[o], 0, [gt[:, e, :] for e in range(2)])
            for item in post:
                if item[0] == "actsB":
                    acts_b_prep()
                elif item[0] == "c0B":
                    c0_prep_b()
                elif item[0] == "half":
                    b_half(item[1], item[2])
        for name, b, part in [["igadd",3,0],["tanh",0,1],["h",0,1]]:
            steps_by_name[name](b, part)

        def gate_mx(b, part, cell):
            n = (NA, P)[part]
            out = {}
            gates_per_bank = 512 // (2 * n)
            if cell == 1 and b == 0 and part == 0:
                banks = []
                for o in range(4):
                    bank = psum.tile([P, 2, n], F32, tag="bank")
                    passes(bank[:, 0, :], 2 * b, GATE_ORDER[o], cell, part, (0, 1))
                    banks.append(bank)
                for o in range(4):
                    passes(banks[o][:, 0, :], 2 * b, GATE_ORDER[o], cell, part, (2,))
                    passes(banks[o][:, 1, :], 2 * b + 1, GATE_ORDER[o], cell, part)
                    out[GATE_ORDER[o]] = [banks[o][:, e, :] for e in range(2)]
                return out
            for g0 in range(0, 4, gates_per_bank):
                bank = psum.tile([P, 2 * gates_per_bank, n], F32, tag="bank")
                for l in range(gates_per_bank):
                    gi = GATE_ORDER[g0 + l]
                    for e in range(2):
                        passes(bank[:, 2 * l + e, :], 2 * b + e, gi, cell, part)
                    out[gi] = [bank[:, 2 * l + e, :] for e in range(2)]
            return out

        for b in range(1, PAIRS):
            if (b, 0) not in ((1, 0),):
                b_half(b, 0)
            if b == 1:
                pair_tanh(PAIRS - 1, 0)
            pair_fc(b, 1, 0)
            if b == PAIRS - 1:
                h1_quantise(0, 1)
            if b == 1:
                pair_h(PAIRS - 1, 0)
            if (b, 1) not in ((1, 0),):
                b_half(b, 1)
            pair_ig_units(b, 1)
            if b == 1:
                h1_interleave(1, 0)
            if b > 1:
                pair_tanh(b - 1, 1)
                pair_h(b - 1, 1)
            pair_add_units(b, 1)
            if b == 1:
                h1_quantise(1, 0)
            if b == 2:
                h1_interleave(0, 1)
        pair_tanh(PAIRS - 1, 1)
        pair_h(PAIRS - 1, 1)
        h1_interleave(1, 1)
        h1_quantise(1, 1)

        def output_transposes(b, part):
            nt = 2 - part
            c_ps = psum.tile([P, nt, 2, P], F32, tag="bank")
            o_ps = psum.tile([P, nt, 2, P], F32, tag="bank")
            for t in range(nt):
                for e in range(2):
                    nc.tensor.transpose(o_ps[:, t, e, :], pa[(b, 3, part)][:, e, 128 * t : 128 * t + 128], ident[:])
            for t in range(nt):
                for e in range(2):
                    nc.tensor.transpose(c_ps[:, t, e, :], c_st[part][:, 2 * b + e, 128 * t : 128 * t + 128], ident[:])
            return c_ps, o_ps

        def output_store(b, part, c_ps, o_ps, who):
            nt = 2 - part
            c_sb = outp.tile([P, nt, 2 * P], F32, tag="c%d" % part)
            h_sb = outp.tile([P, nt, 2 * P], F32, tag="h%d" % part)
            th = outp.tile([P, nt, 2, P], F32, tag="t%d" % part)
            nc.scalar.activation(out=th[:], in_=c_ps[:], func=ACT.Tanh)
            evac(who, c_sb[:].rearrange("p t (m e) -> p t m e", e=2), c_ps[:].rearrange("p t e m -> p t m e"))
            mult(
                h_sb[:].rearrange("p t (m e) -> p t m e", e=2),
                o_ps[:].rearrange("p t e m -> p t m e"),
                th[:].rearrange("p t e m -> p t m e"),
            )
            for dram, sb in ((out_1, c_sb), (out_0, h_sb)):
                if part == 0:
                    nc.sync.dma_start(out=rows_a(dram)[:, :, 256 * b : 256 * b + 256], in_=sb[:])
                else:
                    nc.sync.dma_start(out=rows_b(dram)[:, 256 * b : 256 * b + 256], in_=sb[:, 0, :])

        def vector_store(b, part):
            n = (NA, P)[part]
            pair_tanh(b, part)
            turned = {}
            h = rawp.tile([P, 2 * n], F32, tag="wih", align_bytes=64)
            ct = rawp.tile([P, 2 * n], F32, tag="wih", align_bytes=64)
            ht = rawp.tile([P, 2 * n], F32, tag="wih", align_bytes=64)
            c_sb = outp.tile([P, 2 * n], F32, tag="c%d" % part)
            h_sb = outp.tile([P, 2 * n], F32, tag="h%d" % part)
            nc.vector.transpose(ct[:], c_st[part][:, 2 * b : 2 * b + 2, :].rearrange("p e n -> p (e n)"))
            mult(h[:], pa[(b, 3, part)][:].rearrange("p e n -> p (e n)"), pa[(b, 2, part)][:].rearrange("p e n -> p (e n)"))
            nc.vector.tensor_copy(out=c_sb[:].rearrange("p (m e) -> p m e", e=2), in_=ct[:].rearrange("p (e m) -> p m e", e=2))
            nc.vector.transpose(ht[:], h[:])
            for dram, sb, src in ((out_1, c_sb, None), (out_0, h_sb, ht)):
                if src is not None:
                    nc.vector.tensor_copy(out=sb[:].rearrange("p (m e) -> p m e", e=2), in_=src[:].rearrange("p (e m) -> p m e", e=2))
                rows = dram[0:NA, :].rearrange("(c r t) k -> t r c k", r=32, t=2)
                for q in range(4):
                    lo = 256 * b + 64 * q
                    for t in range(2):
                        nc.sync.dma_start(
                            out=rows[t][:, :, lo : lo + 64],
                            in_=sb[32 * q : 32 * q + 32, 256 * t : 256 * t + 256].rearrange("p (c k) -> p c k", k=64),
                        )

        steps = [(b, part) for b0 in (0, 2) for part in range(2) for b in (b0, b0 + 1)]
        for k, (b, part) in enumerate(steps[:-2]):
            gt = gate_mx(b, part, 1)
            pair_act(b, 1, part, gt[1])
            pair_fc(b, part, 1)
            pair_act(b, 0, part, gt[0])
            pair_act(b, 2, part, gt[2])
            pair_ig_add(b, part)
            pair_act(b, 3, part, gt[3])
            for i in VECTOR_AFTER.get(k, ()):
                vector_store(*steps[i])
            done = [steps[i] for i in OUTPUTS_AFTER.get(k, ())]
            banks = [output_transposes(*step) for step in done]
            for step, (c_ps, o_ps) in zip(done, banks):
                output_store(*step, c_ps, o_ps, "V")

        def gate_bank(*which):
            bank = psum.tile([P, 4, P], F32, tag="bank")
            for l, (b, gi) in enumerate(which):
                for e in range(2):
                    passes(bank[:, 2 * l + e, :], 2 * b + e, gi, 1, 1)
            return [[bank[:, 2 * l + e, :] for e in range(2)] for l in range(2)]

        b0, b1 = PAIRS - 2, PAIRS - 1
        f0, i0 = gate_bank((b0, 1), (b0, 0))
        g0, g1 = gate_bank((b0, 2), (b1, 2))
        f1, i1 = gate_bank((b1, 1), (b1, 0))
        pair_act(b0, 1, 1, f0)
        pair_fc(b0, 1, 1)
        pair_act(b0, 0, 1, i0)
        pair_act(b0, 2, 1, g0)
        pair_ig_add(b0, 1)
        pair_act(b1, 2, 1, g1)
        pair_act(b1, 1, 1, f1)
        pair_fc(b1, 1, 1)
        pair_act(b1, 0, 1, i1)
        pair_ig_add(b1, 1)
        c_ps, o_ps = output_transposes(b1, 0)
        output_store(b1, 0, c_ps, o_ps, "V")
        o0, o1 = gate_bank((b0, 3), (b1, 3))
        pair_act(b0, 3, 1, o0)
        pair_act(b1, 3, 1, o1)
        c_ps = psum.tile([P, 2, 2, P], F32, tag="bank")
        o_ps = psum.tile([P, 2, 2, P], F32, tag="bank")
        for i, b in enumerate((b0, b1)):
            for e in range(2):
                nc.tensor.transpose(c_ps[:, i, e, :], c_st[1][:, 2 * b + e, :], ident[:])
        for i, b in enumerate((b0, b1)):
            for e in range(2):
                nc.tensor.transpose(o_ps[:, i, e, :], pa[(b, 3, 1)][:, e, :], ident[:])
        c_sb = outp.tile([P, 4 * P], F32, tag="c0")
        h_sb = outp.tile([P, 4 * P], F32, tag="h0")
        th = outp.tile([P, 2, 2, P], F32, tag="t0")
        for i in range(2):
            nc.scalar.activation(out=th[:, i], in_=c_ps[:, i], func=ACT.Tanh)
        evac("V", c_sb[:].rearrange("p (i m e) -> p i m e", i=2, e=2), c_ps[:].rearrange("p i e m -> p i m e"))
        nc.sync.dma_start(out=rows_b(out_1)[:, 512:1024], in_=c_sb[:])
        for i in range(2):
            mult(
                h_sb[:, 256 * i : 256 * i + 256].rearrange("p (m e) -> p m e", e=2),
                o_ps[:, i].rearrange("p e m -> p m e"),
                th[:, i].rearrange("p e m -> p m e"),
            )
        nc.sync.dma_start(out=rows_b(out_0)[:, 512:1024], in_=h_sb[:])
